import numpy as np
import ml_dtypes


def mxq(x, axis, fmt="e4m3"):
    dtype, down = {"e4m3": (ml_dtypes.float8_e4m3fn, 7), "e5m2": (ml_dtypes.float8_e5m2, 14)}[fmt]
    v = np.moveaxis(np.asarray(x, np.float32).astype(ml_dtypes.bfloat16).astype(np.float64), axis, -1)
    blocks = v.reshape(v.shape[:-1] + (-1, 32))
    amax = np.abs(blocks).max(-1, keepdims=True)
    byte = np.maximum(np.where(amax > 0, np.frexp(amax)[1] - 1 + 127, 0) - down, 1)
    scale = np.exp2(byte - 127.0)
    codes = (blocks / scale).astype(np.float32).astype(dtype).astype(np.float64)
    return np.moveaxis((codes * scale).reshape(v.shape), -1, axis)


WIDE = False


def mx_kscale(k):
    if not WIDE:
        return np.ones(k)
    levels = np.array([10, -10, 5, -5, 0])
    a = np.random.permutation(np.resize(levels, k // 512 * 4)).reshape(k // 512, 4)
    idx = np.arange(k)
    return np.exp2(a[idx // 512, idx % 128 // 32])


BF16 = ml_dtypes.bfloat16


def bf(x):
    return np.asarray(x, np.float32).astype(BF16)


def f64(x):
    return np.asarray(x).astype(np.float64)


E2M1 = np.array([0.0, 0.5, 1.0, 1.5, 2.0, 3.0, 4.0, 6.0, -0.0, -0.5, -1.0, -1.5, -2.0, -3.0, -4.0, -6.0])


def pack_weight(w, fmt):
    k, n = w.shape
    w = f64(bf(w)).reshape(k // 32, 32, n)
    amax = np.abs(w).max(1)
    if fmt == "e4m3":
        byte = np.frexp(amax)[1] - 1 + 127 - 7
    else:
        mant, ex = np.frexp(amax / 6.0)
        byte = np.where(mant > 0.5, ex, ex - 1) + 127
    byte = np.clip(np.where(amax > 0, byte, 1), 1, 254)
    scaled = (w * np.exp2(127.0 - byte)[:, None, :]).reshape(k, n).astype(np.float32)
    by_word = np.ascontiguousarray(scaled.reshape(k // 512, 128, 4, n).transpose(0, 1, 3, 2))
    if fmt == "e4m3":
        words = by_word.astype(ml_dtypes.float8_e4m3fn).view(np.uint8)
    else:
        c = by_word.astype(ml_dtypes.float4_e2m1fn).view(np.uint8) & 0xF
        words = c[..., 0::2] | (c[..., 1::2] << 4)
    return np.ascontiguousarray(words), np.ascontiguousarray(byte.astype(np.uint8).reshape(k // 512, 16, n))


def unpack_weight(words, scales, fmt):
    g, p, n, _ = words.shape
    if fmt == "e4m3":
        vals = np.ascontiguousarray(words).view(ml_dtypes.float8_e4m3fn).astype(np.float64)
    else:
        nib = np.empty((g, p, n, 4), np.uint8)
        nib[..., 0::2] = words & 0xF
        nib[..., 1::2] = words >> 4
        vals = E2M1[nib]
    vals = vals * np.repeat(np.exp2(scales.astype(np.float64) - 127.0), 8, axis=1)[..., None]
    return vals.transpose(0, 1, 3, 2).reshape(g * 512, n)


N, K, IN, HID, OUT = 128, 2, 2048, 2048, 2048
NEG_SLOPE = 0.01
FMT = "e4m3"


def leaky_relu(v):
    return np.where(v >= 0, v, NEG_SLOPE * v)


def safediv(a, b):
    return a / np.where(b == 0, np.ones_like(b), b)


def setup_inputs():
    s = mx_kscale(IN)
    u = mx_kscale(IN + HID)
    un, t = u[:IN], u[IN:]
    g = np.concatenate([np.full(IN, 1.0), np.full(HID, 3.0)])
    centre = np.random.standard_normal((N, 1, IN))
    h_node = bf(np.random.standard_normal((N, IN)) * un)
    h_ngbrs = bf((0.7 * centre + 0.7 * np.random.standard_normal((N, K, IN))) * s)
    alpha = bf(np.random.uniform(0.0, 1.0, (N, K, 1)))
    Wq = np.random.standard_normal((HID, IN)) / np.sqrt(IN) * t[:, None] / s[None, :]
    bq = bf((-0.5 + 0.3 * np.random.standard_normal(HID)) * t)
    Ww = np.random.standard_normal((OUT, IN + HID)) * g[None, :] / np.sqrt(IN + HID) / u[None, :]
    bw = bf(-0.8 + 0.3 * np.random.standard_normal(OUT))
    Wq_words, Wq_scales = pack_weight(np.ascontiguousarray(Wq.T), FMT)
    Ww_words, Ww_scales = pack_weight(np.ascontiguousarray(Ww.T), FMT)
    return {"h_node": h_node,
            "h_ngbrs": h_ngbrs,
            "alpha": alpha,
            "Wq_words": Wq_words,
            "Wq_scales": Wq_scales,
            "bq": bq,
            "Ww_words": Ww_words,
            "Ww_scales": Ww_scales,
            "bw": bw}


def reference(h_node, h_ngbrs, alpha, Wq_words, Wq_scales, bq, Ww_words, Ww_scales, bw):
    a = f64(alpha)
    h1 = leaky_relu((mxq(f64(h_ngbrs), 2, "e4m3") @ unpack_weight(Wq_words, Wq_scales, FMT)) + f64(bq))
    h_agg = safediv((a * h1).sum(axis=1), a.sum(axis=1))
    h_concat = np.concatenate([f64(h_node), h_agg], axis=-1)
    h2 = leaky_relu((mxq(h_concat, 1, "e4m3") @ unpack_weight(Ww_words, Ww_scales, FMT)) + f64(bw))
    nrm = np.sqrt((h2 ** 2).sum(axis=-1, keepdims=True))
    return safediv(h2, nrm)

@@ -1,0 +1,308 @@
+from contextlib import ExitStack
+
+import concourse.bass as bass
+import concourse.mybir as mybir
+import concourse.tile as tile
+from concourse.masks import make_identity
+
+F32 = mybir.dt.float32
+BF16 = mybir.dt.bfloat16
+I32 = mybir.dt.int32
+U32 = mybir.dt.uint32
+U8 = mybir.dt.uint8
+FP8X4 = mybir.dt.float8_e4m3fn_x4
+ALU = mybir.AluOpType
+ACT = mybir.ActivationFunctionType
+
+P = 128
+FEAT = 2048
+NB = 2
+K_PASS = 512
+GQ = FEAT // K_PASS
+GW = 2 * FEAT // K_PASS
+NT = 512
+HALF = 1024
+PART1 = 1536
+SLOPE = 0.01
+TINY = 1e-30
+PIN = False
+
+FLOPS = 2 * P * NB * FEAT * FEAT + 2 * P * 2 * FEAT * FEAT
+
+
+def tile_pinsageconv_w_kernel(tc, h_node, h_ngbrs, alpha, Wq_words, Wq_scales, bq, Ww_words, Ww_scales, bw, out):
+    nc = tc.nc
+    with ExitStack() as ctx:
+        if PIN:
+            ctx.enter_context(tc.manual_schedule())
+        keep = ctx.enter_context(tc.tile_pool(name="keep", bufs=1))
+        work = ctx.enter_context(tc.tile_pool(name="work", bufs=2))
+        psum = ctx.enter_context(tc.psum_pool(name="psum", bufs=1))
+
+        def bank(i, shape, dtype, name):
+            return psum.tile(shape, dtype, tag="bank%d" % i, name=name)
+
+        wq = keep.tile([P, GQ, FEAT], I32, align_bytes=64)
+        ww = keep.tile([P, GW, FEAT], I32, align_bytes=64)
+        wq_pl = keep.tile([P, FEAT], U8, align_bytes=64)
+        ww_pl = keep.tile([P, 2, FEAT], U8, align_bytes=64)
+        xn = keep.tile([P, NB, FEAT], BF16, align_bytes=64)
+        xh = keep.tile([P, FEAT], BF16, align_bytes=64)
+        gx = keep.tile([P, NB * GQ, P, 4], BF16, align_bytes=64)
+        gh = keep.tile([P, GQ, P, 4], BF16, align_bytes=64)
+        ga = keep.tile([P, GQ, P, 4], BF16, align_bytes=64)
+        cx = keep.tile([P, NB * GQ * P], U32, align_bytes=64)
+        ch = keep.tile([P, GQ * P], U32, align_bytes=64)
+        ca = keep.tile([P, GQ * P], U32, align_bytes=64)
+        px = keep.tile([P, NB * GQ * P], U8, align_bytes=64)
+        ph = keep.tile([P, GQ * P], U8, align_bytes=64)
+        pa = keep.tile([P, GQ * P], U8, align_bytes=64)
+        ident_f = keep.tile([P, P], F32)
+        ident_b = keep.tile([P, P], BF16)
+        brow = keep.tile([P, NT], BF16)
+        bias_b = keep.tile([P, 2 * FEAT], F32)
+        a_bf = keep.tile([P, NB], BF16)
+        a_f = keep.tile([P, NB], F32)
+        a_sum = keep.tile([P, 1], F32)
+        a_safe = keep.tile([P, 1], F32)
+        a_rec = keep.tile([P, 1], F32)
+        wgt = keep.tile([P, NB], F32)
+        one = keep.tile([P, 1], F32)
+        warm = keep.tile([P, 1], F32)
+        hagg = keep.tile([P, FEAT], BF16)
+        h2 = keep.tile([P, FEAT], F32)
+        res = keep.tile([P, FEAT], F32)
+        ssp = keep.tile([P, 4], F32)
+        ss01 = keep.tile([P, 1], F32)
+        ssprev = keep.tile([P, 1], F32)
+        rn = keep.tile([P, 1], F32)
+
+        nc.vector.memset(wq_pl[:].bitcast(I32), 0)
+        nc.vector.memset(brow[:], 0.0)
+        nc.vector.memset(one[:], 1.0)
+        nc.vector.memset(ww_pl[:].rearrange("p h n -> p (h n)").bitcast(I32), 0)
+        make_identity(nc, ident_f[:])
+        make_identity(nc, ident_b[:])
+
+        nc.scalar.dma_start(out=brow[0:4, :], in_=bq.rearrange("(c n) -> c n", c=4))
+        nc.scalar.dma_start(out=brow[4:8, :], in_=bw.rearrange("(c n) -> c n", c=4))
+        nc.scalar.dma_start(out=a_bf[:], in_=alpha.rearrange("n k o -> n (k o)"))
+        nc.scalar.activation(out=warm[:], in_=one[:], func=ACT.Abs_reciprocal_sqrt)
+
+        for kk in range(NB):
+            nc.sync.dma_start(out=xn[:, kk, :], in_=h_ngbrs[:, kk, :])
+        for q in (0, 2, 1, 3):
+            nc.sync.dma_start(
+                out=wq_pl[32 * q : 32 * q + 16, :].bitcast(I32),
+                in_=Wq_scales[:, 4 * q : 4 * q + 4, :].bitcast(I32),
+            )
+        for h in range(2):
+            for g in range(GQ):
+                nc.sync.dma_start(
+                    out=wq[:, g, h * HALF : (h + 1) * HALF],
+                    in_=Wq_words[g, :, h * HALF : (h + 1) * HALF, :].rearrange("p n t -> p (n t)").bitcast(I32),
+                )
+        nc.sync.dma_start(out=xh[:], in_=h_node)
+        for hh in range(2):
+            for q in (0, 2, 1, 3):
+                nc.sync.dma_start(
+                    out=ww_pl[32 * q : 32 * q + 16, hh, :].bitcast(I32),
+                    in_=Ww_scales[4 * hh : 4 * hh + 4, 4 * q : 4 * q + 4, :].bitcast(I32),
+                )
+        for g in range(GW):
+            nc.sync.dma_start(
+                out=ww[:, g, 0:PART1],
+                in_=Ww_words[g, :, 0:PART1, :].rearrange("p n t -> p (n t)").bitcast(I32),
+            )
+        for g in range(GW):
+            nc.sync.dma_start(
+                out=ww[:, g, PART1:FEAT],
+                in_=Ww_words[g, :, PART1:FEAT, :].rearrange("p n t -> p (n t)").bitcast(I32),
+            )
+
+        def bias_matmul(j, b):
+            pb = bank(b, [P, NT], F32, "pb%d" % j)
+            nc.tensor.matmul(out=pb[:], lhsT=ident_b[:, j : j + 1].to_broadcast([P, P]), rhs=brow[:], start=True, stop=True)
+            return pb
+
+        def bias_evac(j, pb):
+            nc.scalar.copy(out=bias_b[:, j * NT : (j + 1) * NT], in_=pb[:])
+
+        def word_transposes(src_words, b, unit0, name):
+            pt = bank(b, [P, 2, 2, P], F32, name)
+            for a in range(2):
+                base = 256 * (unit0 + a)
+                for u in range(2):
+                    nc.tensor.transpose(pt[:, a, u, :], src_words[:, base + u : base + 256 : 2], ident_f[:])
+            return pt
+
+        def word_evac(eng_copy, dst, unit0, pt):
+            eng_copy(
+                out=dst[:, unit0 : unit0 + 2, :, :].bitcast(F32),
+                in_=pt[:].rearrange("p a u r -> p a r u"),
+            )
+
+        def quantise(src, codes, plane, unit0, units):
+            nc.vector.quantize_mx(
+                out=codes[:, unit0 * P : (unit0 + units) * P].bitcast(FP8X4),
+                scales=plane[:, unit0 * P : (unit0 + units) * P],
+                in_=src[:, unit0 : unit0 + units, :, :].rearrange("p a r t -> p (a r t)"),
+            )
+
+        pbs = [bias_matmul(j, 4 + j) for j in range(4)]
+        bias_evac(0, pbs[0])
+        bias_evac(1, pbs[1])
+        xnw = xn[:].rearrange("p k f -> p (k f)").bitcast(F32)
+        t0 = word_transposes(xnw, 0, 0, "t0")
+        t1 = word_transposes(xnw, 1, 2, "t1")
+        word_evac(nc.vector.tensor_copy, gx, 0, t0)
+        word_evac(nc.scalar.copy, gx, 2, t1)
+        bias_evac(2, pbs[2])
+        bias_evac(3, pbs[3])
+        t2 = word_transposes(xnw, 2, 4, "t2")
+        t3 = word_transposes(xnw, 3, 6, "t3")
+        word_evac(nc.vector.tensor_copy, gx, 4, t2)
+        word_evac(nc.scalar.copy, gx, 6, t3)
+        quantise(gx, cx, px, 0, 4)
+        quantise(gx, cx, px, 4, 4)
+
+        nc.vector.tensor_copy(out=a_f[:], in_=a_bf[:])
+        nc.vector.tensor_tensor(out=a_sum[:], in0=a_f[:, 0:1], in1=a_f[:, 1:2], op=ALU.add)
+        nc.vector.scalar_tensor_tensor(out=a_safe[:], in0=a_sum[:], scalar=0.0, in1=a_sum[:], op0=ALU.is_equal, op1=ALU.add)
+        nc.vector.reciprocal(out=a_rec[:], in_=a_safe[:])
+        nc.vector.tensor_scalar(out=wgt[:], in0=a_f[:], scalar1=a_rec[:, 0:1], scalar2=None, op0=ALU.mult)
+
+        pbs2 = [bias_matmul(4 + j, 4 + j) for j in range(4)]
+        for j in range(4):
+            bias_evac(4 + j, pbs2[j])
+
+        acc1 = {}
+        for h in range(2):
+            for kk in range(NB):
+                for cc in range(2):
+                    acc1[(h, kk, cc)] = bank(4 * h + 2 * kk + cc, [P, NT], F32, "acc1_%d%d%d" % (h, kk, cc))
+            for g in range(GQ):
+                for kk in range(NB):
+                    unit = kk * GQ + g
+                    for cc in range(2):
+                        c0 = h * HALF + cc * NT
+                        nc.tensor.matmul_mx(
+                            out=acc1[(h, kk, cc)][:],
+                            lhsT=cx[:, unit * P : (unit + 1) * P].bitcast(FP8X4),
+                            lhsT_scale=px[:, unit * P : (unit + 1) * P],
+                            rhs=wq[:, g, c0 : c0 + NT].bitcast(FP8X4),
+                            rhs_scale=wq_pl[4 * g : P, c0 : c0 + NT],
+                            start=(g == 0),
+                            stop=(g == GQ - 1),
+                        )
+
+        def add_bias1(h, kk, v):
+            for cc in range(2):
+                c0 = h * HALF + cc * NT
+                nc.vector.tensor_tensor(out=v[:, cc * NT : (cc + 1) * NT], in0=acc1[(h, kk, cc)][:], in1=bias_b[:, c0 : c0 + NT], op=ALU.add)
+
+        def lrelu(dst, v):
+            nc.vector.scalar_tensor_tensor(out=dst, in0=v, scalar=SLOPE, in1=v, op0=ALU.mult, op1=ALU.max)
+
+        def agg_transposes(gp, b):
+            pt = bank(b, [P, 4, P], BF16, "ta%d" % gp)
+            for t in range(4):
+                nc.tensor.transpose(pt[:, t, :], hagg[:, K_PASS * gp + t : K_PASS * (gp + 1) : 4], ident_b[:])
+            return pt
+
+        def agg_evac(eng_copy, gp, pt):
+            eng_copy(out=ga[:, gp, :, :], in_=pt[:].rearrange("p t r -> p r t"))
+
+        v00 = work.tile([P, HALF], F32, tag="v0")
+        u00 = work.tile([P, HALF], F32, tag="u0")
+        v01 = work.tile([P, HALF], F32, tag="v1")
+        u01 = work.tile([P, HALF], F32, tag="u1")
+        y0 = work.tile([P, HALF], F32, tag="y")
+        add_bias1(0, 0, v00)
+        lrelu(u00[:], v00[:])
+        nc.scalar.activation(out=y0[:], in_=u00[:], func=ACT.Copy, scale=wgt[:, 0:1])
+        add_bias1(0, 1, v01)
+        lrelu(u01[:], v01[:])
+        nc.vector.scalar_tensor_tensor(out=hagg[:, 0:HALF], in0=u01[:], scalar=wgt[:, 1:2], in1=y0[:], op0=ALU.mult, op1=ALU.add)
+
+        xhw = xh[:].bitcast(F32)
+        t4 = word_transposes(xhw, 0, 0, "t4")
+        t5 = word_transposes(xhw, 1, 2, "t5")
+        word_evac(nc.scalar.copy, gh, 0, t4)
+        word_evac(nc.scalar.copy, gh, 2, t5)
+
+        v10 = work.tile([P, HALF], F32, tag="v0")
+        u10 = work.tile([P, HALF], F32, tag="u0")
+        v11 = work.tile([P, HALF], F32, tag="v1")
+        u11 = work.tile([P, HALF], F32, tag="u1")
+        y1 = work.tile([P, HALF], F32, tag="y")
+        add_bias1(1, 0, v10)
+        lrelu(u10[:], v10[:])
+        ta0 = agg_transposes(0, 4)
+        ta1 = agg_transposes(1, 5)
+        agg_evac(nc.scalar.copy, 0, ta0)
+        agg_evac(nc.scalar.copy, 1, ta1)
+        nc.scalar.activation(out=y1[:], in_=u10[:], func=ACT.Copy, scale=wgt[:, 0:1])
+        quantise(gh, ch, ph, 0, 4)
+        add_bias1(1, 1, v11)
+        quantise(ga, ca, pa, 0, 2)
+        lrelu(u11[:], v11[:])
+        nc.vector.scalar_tensor_tensor(out=hagg[:, HALF:FEAT], in0=u11[:], scalar=wgt[:, 1:2], in1=y1[:], op0=ALU.mult, op1=ALU.add)
+
+        acc2 = [bank(c, [P, NT], F32, "acc2_%d" % c) for c in range(4)]
+
+        def pass2(g, c):
+            if g < GQ:
+                codes, plane, unit = ch, ph, g
+            else:
+                codes, plane, unit = ca, pa, g - GQ
+            nc.tensor.matmul_mx(
+                out=acc2[c][:],
+                lhsT=codes[:, unit * P : (unit + 1) * P].bitcast(FP8X4),
+                lhsT_scale=plane[:, unit * P : (unit + 1) * P],
+                rhs=ww[:, g, c * NT : (c + 1) * NT].bitcast(FP8X4),
+                rhs_scale=ww_pl[4 * (g % 4) : P, g // 4, c * NT : (c + 1) * NT],
+                start=(g == 0),
+                stop=(g == GW - 1),
+            )
+
+        for g in range(2):
+            for c in range(3):
+                pass2(g, c)
+        ta2 = agg_transposes(2, 6)
+        ta3 = agg_transposes(3, 7)
+        agg_evac(nc.scalar.copy, 2, ta2)
+        agg_evac(nc.vector.tensor_copy, 3, ta3)
+        quantise(ga, ca, pa, 2, 2)
+        for g in range(2, GW):
+            for c in range(3):
+                pass2(g, c)
+        for g in range(GW):
+            pass2(g, 3)
+
+        junk = keep.tile([P, NT], F32)
+
+        def epilogue2(c):
+            cols = slice(c * NT, (c + 1) * NT)
+            v = work.tile([P, NT], F32, tag="v2")
+            nc.vector.tensor_tensor(out=v[:], in0=acc2[c][:], in1=bias_b[:, FEAT + c * NT : FEAT + (c + 1) * NT], op=ALU.add)
+            lrelu(h2[:, cols], v[:])
+            nc.scalar.activation(out=junk[:], in_=h2[:, cols], func=ACT.Square, accum_out=ssp[:, c : c + 1])
+
+        for c in range(3):
+            epilogue2(c)
+        nc.vector.tensor_tensor(out=ss01[:], in0=ssp[:, 0:1], in1=ssp[:, 1:2], op=ALU.add)
+        nc.vector.scalar_tensor_tensor(out=ssprev[:], in0=ssp[:, 2:3], scalar=TINY, in1=ss01[:], op0=ALU.add, op1=ALU.add)
+        epilogue2(3)
+        nc.scalar.activation(out=rn[:], in_=ssp[:, 3:4], func=ACT.Abs_reciprocal_sqrt, bias=ssprev[:, 0:1], scale=1.0)
+
+        def scale_v(c):
+            cols = slice(c * NT, (c + 1) * NT)
+            nc.vector.tensor_scalar(out=res[:, cols], in0=h2[:, cols], scalar1=rn[:, 0:1], scalar2=None, op0=ALU.mult)
+            nc.sync.dma_start(out=out[:, cols], in_=res[:, cols])
+
+        scale_v(0)
+        nc.scalar.activation(out=res[:, 2 * NT : 3 * NT], in_=h2[:, 2 * NT : 3 * NT], func=ACT.Copy, scale=rn[:, 0:1])
+        nc.sync.dma_start(out=out[:, 2 * NT : 3 * NT], in_=res[:, 2 * NT : 3 * NT])
+        scale_v(1)
+        scale_v(3)

@@ -81,8 +81,19 @@ def tile_pinsageconv_w_kernel(tc, h_node, h_ngbrs, alpha, Wq_words, Wq_scales, b
         nc.vector.memset(brow[:], 0.0)
         nc.vector.memset(one[:], 1.0)
         nc.vector.memset(ww_pl[:].rearrange("p h n -> p (h n)").bitcast(I32), 0)
+        for q in (0, 2, 1, 3):
+            nc.gpsimd.dma_start(
+                out=wq_pl[32 * q : 32 * q + 16, :].bitcast(F32),
+                in_=Wq_scales[:, 4 * q : 4 * q + 4, :].bitcast(F32),
+            )
         make_identity(nc, ident_f[:])
         make_identity(nc, ident_b[:])
+        for hh in range(2):
+            for q in (0, 2, 1, 3):
+                nc.gpsimd.dma_start(
+                    out=ww_pl[32 * q : 32 * q + 16, hh, :].bitcast(F32),
+                    in_=Ww_scales[4 * hh : 4 * hh + 4, 4 * q : 4 * q + 4, :].bitcast(F32),
+                )
 
         nc.scalar.dma_start(out=brow[0:4, :], in_=bq.rearrange("(c n) -> c n", c=4))
         nc.scalar.dma_start(out=brow[4:8, :], in_=bw.rearrange("(c n) -> c n", c=4))
@@ -91,11 +102,6 @@ def tile_pinsageconv_w_kernel(tc, h_node, h_ngbrs, alpha, Wq_words, Wq_scales, b
 
         for kk in range(NB):
             nc.sync.dma_start(out=xn[:, kk, :], in_=h_ngbrs[:, kk, :])
-        for q in (0, 2, 1, 3):
-            nc.sync.dma_start(
-                out=wq_pl[32 * q : 32 * q + 16, :].bitcast(I32),
-                in_=Wq_scales[:, 4 * q : 4 * q + 4, :].bitcast(I32),
-            )
         for h in range(2):
             for g in range(GQ):
                 nc.sync.dma_start(
@@ -103,12 +109,6 @@ def tile_pinsageconv_w_kernel(tc, h_node, h_ngbrs, alpha, Wq_words, Wq_scales, b
                     in_=Wq_words[g, :, h * HALF : (h + 1) * HALF, :].rearrange("p n t -> p (n t)").bitcast(I32),
                 )
         nc.sync.dma_start(out=xh[:], in_=h_node)
-        for hh in range(2):
-            for q in (0, 2, 1, 3):
-                nc.sync.dma_start(
-                    out=ww_pl[32 * q : 32 * q + 16, hh, :].bitcast(I32),
-                    in_=Ww_scales[4 * hh : 4 * hh + 4, 4 * q : 4 * q + 4, :].bitcast(I32),
-                )
         for g in range(GW):
             nc.sync.dma_start(
                 out=ww[:, g, 0:PART1],

@@ -81,44 +81,59 @@ def tile_pinsageconv_w_kernel(tc, h_node, h_ngbrs, alpha, Wq_words, Wq_scales, b
         nc.vector.memset(brow[:], 0.0)
         nc.vector.memset(one[:], 1.0)
         nc.vector.memset(ww_pl[:].rearrange("p h n -> p (h n)").bitcast(I32), 0)
-        for q in (0, 2, 1, 3):
-            nc.gpsimd.dma_start(
-                out=wq_pl[32 * q : 32 * q + 16, :].bitcast(F32),
-                in_=Wq_scales[:, 4 * q : 4 * q + 4, :].bitcast(F32),
-            )
         make_identity(nc, ident_f[:])
         make_identity(nc, ident_b[:])
-        for hh in range(2):
-            for q in (0, 2, 1, 3):
-                nc.gpsimd.dma_start(
-                    out=ww_pl[32 * q : 32 * q + 16, hh, :].bitcast(F32),
-                    in_=Ww_scales[4 * hh : 4 * hh + 4, 4 * q : 4 * q + 4, :].bitcast(F32),
-                )
 
         nc.scalar.dma_start(out=brow[0:4, :], in_=bq.rearrange("(c n) -> c n", c=4))
         nc.scalar.dma_start(out=brow[4:8, :], in_=bw.rearrange("(c n) -> c n", c=4))
         nc.scalar.dma_start(out=a_bf[:], in_=alpha.rearrange("n k o -> n (k o)"))
         nc.scalar.activation(out=warm[:], in_=one[:], func=ACT.Abs_reciprocal_sqrt)
 
-        for kk in range(NB):
-            nc.sync.dma_start(out=xn[:, kk, :], in_=h_ngbrs[:, kk, :])
-        for h in range(2):
-            for g in range(GQ):
-                nc.sync.dma_start(
-                    out=wq[:, g, h * HALF : (h + 1) * HALF],
-                    in_=Wq_words[g, :, h * HALF : (h + 1) * HALF, :].rearrange("p n t -> p (n t)").bitcast(I32),
-                )
+        def load_wq_plane(q):
+            nc.sync.dma_start(
+                out=wq_pl[32 * q : 32 * q + 16, :].bitcast(I32),
+                in_=Wq_scales[:, 4 * q : 4 * q + 4, :].bitcast(I32),
+            )
+
+        def load_ww_plane(i):
+            hh, q = i // 4, (0, 2, 1, 3)[i % 4]
+            nc.sync.dma_start(
+                out=ww_pl[32 * q : 32 * q + 16, hh, :].bitcast(I32),
+                in_=Ww_scales[4 * hh : 4 * hh + 4, 4 * q : 4 * q + 4, :].bitcast(I32),
+            )
+
+        def load_wq(h, g):
+            nc.sync.dma_start(
+                out=wq[:, g, h * HALF : (h + 1) * HALF],
+                in_=Wq_words[g, :, h * HALF : (h + 1) * HALF, :].rearrange("p n t -> p (n t)").bitcast(I32),
+            )
+
+        def load_ww(g, lo, hi):
+            nc.sync.dma_start(
+                out=ww[:, g, lo:hi],
+                in_=Ww_words[g, :, lo:hi, :].rearrange("p n t -> p (n t)").bitcast(I32),
+            )
+
+        nc.sync.dma_start(out=xn[:].rearrange("p k f -> p (k f)"), in_=h_ngbrs.rearrange("n k f -> n (k f)"))
+        for q in (0, 2, 1, 3):
+            load_wq_plane(q)
+        for g in range(3):
+            load_wq(0, g)
+        load_wq(0, 3)
+        load_ww_plane(0)
+        for g in range(GQ):
+            load_wq(1, g)
+            load_ww_plane(1 + g)
         nc.sync.dma_start(out=xh[:], in_=h_node)
+        load_ww_plane(5)
+        load_ww(0, 0, PART1)
+        load_ww_plane(6)
+        load_ww(1, 0, PART1)
+        load_ww_plane(7)
+        for g in range(2, GW):
+            load_ww(g, 0, PART1)
         for g in range(GW):
-            nc.sync.dma_start(
-                out=ww[:, g, 0:PART1],
-                in_=Ww_words[g, :, 0:PART1, :].rearrange("p n t -> p (n t)").bitcast(I32),
-            )
-        for g in range(GW):
-            nc.sync.dma_start(
-                out=ww[:, g, PART1:FEAT],
-                in_=Ww_words[g, :, PART1:FEAT, :].rearrange("p n t -> p (n t)").bitcast(I32),
-            )
+            load_ww(g, PART1, FEAT)
 
         def bias_matmul(j, b):
             pb = bank(b, [P, NT], F32, "pb%d" % j)

@@ -25,7 +25,7 @@ HALF = 1024
 PART1 = 1536
 SLOPE = 0.01
 TINY = 1e-30
-PIN = False
+PIN = True
 
 FLOPS = 2 * P * NB * FEAT * FEAT + 2 * P * 2 * FEAT * FEAT
 
@@ -89,51 +89,36 @@ def tile_pinsageconv_w_kernel(tc, h_node, h_ngbrs, alpha, Wq_words, Wq_scales, b
         nc.scalar.dma_start(out=a_bf[:], in_=alpha.rearrange("n k o -> n (k o)"))
         nc.scalar.activation(out=warm[:], in_=one[:], func=ACT.Abs_reciprocal_sqrt)
 
-        def load_wq_plane(q):
+        for kk in range(NB):
+            nc.sync.dma_start(out=xn[:, kk, :], in_=h_ngbrs[:, kk, :])
+        for q in (0, 2, 1, 3):
             nc.sync.dma_start(
                 out=wq_pl[32 * q : 32 * q + 16, :].bitcast(I32),
                 in_=Wq_scales[:, 4 * q : 4 * q + 4, :].bitcast(I32),
             )
-
-        def load_ww_plane(i):
-            hh, q = i // 4, (0, 2, 1, 3)[i % 4]
-            nc.sync.dma_start(
-                out=ww_pl[32 * q : 32 * q + 16, hh, :].bitcast(I32),
-                in_=Ww_scales[4 * hh : 4 * hh + 4, 4 * q : 4 * q + 4, :].bitcast(I32),
-            )
-
-        def load_wq(h, g):
-            nc.sync.dma_start(
-                out=wq[:, g, h * HALF : (h + 1) * HALF],
-                in_=Wq_words[g, :, h * HALF : (h + 1) * HALF, :].rearrange("p n t -> p (n t)").bitcast(I32),
-            )
-
-        def load_ww(g, lo, hi):
-            nc.sync.dma_start(
-                out=ww[:, g, lo:hi],
-                in_=Ww_words[g, :, lo:hi, :].rearrange("p n t -> p (n t)").bitcast(I32),
-            )
-
-        nc.sync.dma_start(out=xn[:].rearrange("p k f -> p (k f)"), in_=h_ngbrs.rearrange("n k f -> n (k f)"))
-        for q in (0, 2, 1, 3):
-            load_wq_plane(q)
-        for g in range(3):
-            load_wq(0, g)
-        load_wq(0, 3)
-        load_ww_plane(0)
-        for g in range(GQ):
-            load_wq(1, g)
-            load_ww_plane(1 + g)
+        for h in range(2):
+            for g in range(GQ):
+                nc.sync.dma_start(
+                    out=wq[:, g, h * HALF : (h + 1) * HALF],
+                    in_=Wq_words[g, :, h * HALF : (h + 1) * HALF, :].rearrange("p n t -> p (n t)").bitcast(I32),
+                )
         nc.sync.dma_start(out=xh[:], in_=h_node)
-        load_ww_plane(5)
-        load_ww(0, 0, PART1)
-        load_ww_plane(6)
-        load_ww(1, 0, PART1)
-        load_ww_plane(7)
-        for g in range(2, GW):
-            load_ww(g, 0, PART1)
+        for hh in range(2):
+            for q in (0, 2, 1, 3):
+                nc.sync.dma_start(
+                    out=ww_pl[32 * q : 32 * q + 16, hh, :].bitcast(I32),
+                    in_=Ww_scales[4 * hh : 4 * hh + 4, 4 * q : 4 * q + 4, :].bitcast(I32),
+                )
         for g in range(GW):
-            load_ww(g, PART1, FEAT)
+            nc.sync.dma_start(
+                out=ww[:, g, 0:PART1],
+                in_=Ww_words[g, :, 0:PART1, :].rearrange("p n t -> p (n t)").bitcast(I32),
+            )
+        for g in range(GW):
+            nc.sync.dma_start(
+                out=ww[:, g, PART1:FEAT],
+                in_=Ww_words[g, :, PART1:FEAT, :].rearrange("p n t -> p (n t)").bitcast(I32),
+            )
 
         def bias_matmul(j, b):
             pb = bank(b, [P, NT], F32, "pb%d" % j)

@@ -22,10 +22,11 @@ GQ = FEAT // K_PASS
 GW = 2 * FEAT // K_PASS
 NT = 512
 HALF = 1024
-PART1 = 1536
+SPLIT = (512, 1024, 1024, 1536, 1536, 1792, 1792, 1792)
+GROUPS = ((0, 512), (512, 1024), (1024, 1536), (1536, 1792), (1792, 2048))
 SLOPE = 0.01
 TINY = 1e-30
-PIN = True
+PIN = False
 
 FLOPS = 2 * P * NB * FEAT * FEAT + 2 * P * 2 * FEAT * FEAT
 
@@ -72,7 +73,7 @@ def tile_pinsageconv_w_kernel(tc, h_node, h_ngbrs, alpha, Wq_words, Wq_scales, b
         hagg = keep.tile([P, FEAT], BF16)
         h2 = keep.tile([P, FEAT], F32)
         res = keep.tile([P, FEAT], F32)
-        ssp = keep.tile([P, 4], F32)
+        ssp = keep.tile([P, 5], F32)
         ss01 = keep.tile([P, 1], F32)
         ssprev = keep.tile([P, 1], F32)
         rn = keep.tile([P, 1], F32)
@@ -109,15 +110,11 @@ def tile_pinsageconv_w_kernel(tc, h_node, h_ngbrs, alpha, Wq_words, Wq_scales, b
                     out=ww_pl[32 * q : 32 * q + 16, hh, :].bitcast(I32),
                     in_=Ww_scales[4 * hh : 4 * hh + 4, 4 * q : 4 * q + 4, :].bitcast(I32),
                 )
-        for g in range(GW):
+        pieces = [(g, 0, SPLIT[g]) for g in range(GW)] + [(g, SPLIT[g], FEAT) for g in range(GW)]
+        for g, lo, hi in pieces:
             nc.sync.dma_start(
-                out=ww[:, g, 0:PART1],
-                in_=Ww_words[g, :, 0:PART1, :].rearrange("p n t -> p (n t)").bitcast(I32),
-            )
-        for g in range(GW):
-            nc.sync.dma_start(
-                out=ww[:, g, PART1:FEAT],
-                in_=Ww_words[g, :, PART1:FEAT, :].rearrange("p n t -> p (n t)").bitcast(I32),
+                out=ww[:, g, lo:hi],
+                in_=Ww_words[g, :, lo:hi, :].rearrange("p n t -> p (n t)").bitcast(I32),
             )
 
         def bias_matmul(j, b):
@@ -249,52 +246,56 @@ def tile_pinsageconv_w_kernel(tc, h_node, h_ngbrs, alpha, Wq_words, Wq_scales, b
         lrelu(u11[:], v11[:])
         nc.vector.scalar_tensor_tensor(out=hagg[:, HALF:FEAT], in0=u11[:], scalar=wgt[:, 1:2], in1=y1[:], op0=ALU.mult, op1=ALU.add)
 
-        acc2 = [bank(c, [P, NT], F32, "acc2_%d" % c) for c in range(4)]
+        acc2 = [bank(j, [P, hi - lo], F32, "acc2_%d" % j) for j, (lo, hi) in enumerate(GROUPS)]
+        todo = []
+        for g, lo, hi in pieces:
+            for j, (glo, ghi) in enumerate(GROUPS):
+                if lo <= glo and ghi <= hi:
+                    todo.append((g, j))
+        seen = [0] * len(GROUPS)
 
-        def pass2(g, c):
+        def pass2(g, j):
+            lo, hi = GROUPS[j]
             if g < GQ:
                 codes, plane, unit = ch, ph, g
             else:
                 codes, plane, unit = ca, pa, g - GQ
             nc.tensor.matmul_mx(
-                out=acc2[c][:],
+                out=acc2[j][:],
                 lhsT=codes[:, unit * P : (unit + 1) * P].bitcast(FP8X4),
                 lhsT_scale=plane[:, unit * P : (unit + 1) * P],
-                rhs=ww[:, g, c * NT : (c + 1) * NT].bitcast(FP8X4),
-                rhs_scale=ww_pl[4 * (g % 4) : P, g // 4, c * NT : (c + 1) * NT],
-                start=(g == 0),
-                stop=(g == GW - 1),
+                rhs=ww[:, g, lo:hi].bitcast(FP8X4),
+                rhs_scale=ww_pl[4 * (g % 4) : P, g // 4, lo:hi],
+                start=(seen[j] == 0),
+                stop=(seen[j] == GW - 1),
             )
+            seen[j] += 1
 
-        for g in range(2):
-            for c in range(3):
-                pass2(g, c)
+        for g, j in todo[:3]:
+            pass2(g, j)
         ta2 = agg_transposes(2, 6)
         ta3 = agg_transposes(3, 7)
         agg_evac(nc.scalar.copy, 2, ta2)
         agg_evac(nc.vector.tensor_copy, 3, ta3)
         quantise(ga, ca, pa, 2, 2)
-        for g in range(2, GW):
-            for c in range(3):
-                pass2(g, c)
-        for g in range(GW):
-            pass2(g, 3)
+        for g, j in todo[3:]:
+            pass2(g, j)
 
         junk = keep.tile([P, NT], F32)
 
-        def epilogue2(c):
-            cols = slice(c * NT, (c + 1) * NT)
+        def epilogue2(j):
+            lo, hi = GROUPS[j]
             v = work.tile([P, NT], F32, tag="v2")
-            nc.vector.tensor_tensor(out=v[:], in0=acc2[c][:], in1=bias_b[:, FEAT + c * NT : FEAT + (c + 1) * NT], op=ALU.add)
-            lrelu(h2[:, cols], v[:])
-            nc.scalar.activation(out=junk[:], in_=h2[:, cols], func=ACT.Square, accum_out=ssp[:, c : c + 1])
+            nc.vector.tensor_tensor(out=v[:, 0 : hi - lo], in0=acc2[j][:], in1=bias_b[:, FEAT + lo : FEAT + hi], op=ALU.add)
+            lrelu(h2[:, lo:hi], v[:, 0 : hi - lo])
+            nc.scalar.activation(out=junk[:, 0 : hi - lo], in_=h2[:, lo:hi], func=ACT.Square, accum_out=ssp[:, j : j + 1])
 
-        for c in range(3):
-            epilogue2(c)
-        nc.vector.tensor_tensor(out=ss01[:], in0=ssp[:, 0:1], in1=ssp[:, 1:2], op=ALU.add)
-        nc.vector.scalar_tensor_tensor(out=ssprev[:], in0=ssp[:, 2:3], scalar=TINY, in1=ss01[:], op0=ALU.add, op1=ALU.add)
-        epilogue2(3)
-        nc.scalar.activation(out=rn[:], in_=ssp[:, 3:4], func=ACT.Abs_reciprocal_sqrt, bias=ssprev[:, 0:1], scale=1.0)
+        for j in range(4):
+            epilogue2(j)
+        epilogue2(4)
+        nc.vector.tensor_reduce(out=ss01[:], in_=ssp[:, 0:4], op=ALU.add, axis=mybir.AxisListType.X)
+        nc.vector.tensor_scalar(out=ssprev[:], in0=ss01[:], scalar1=TINY, scalar2=None, op0=ALU.add)
+        nc.scalar.activation(out=rn[:], in_=ssp[:, 4:5], func=ACT.Abs_reciprocal_sqrt, bias=ssprev[:, 0:1], scale=1.0)
 
         def scale_v(c):
             cols = slice(c * NT, (c + 1) * NT)

@@ -21,7 +21,12 @@ K_PASS = 512
 GQ = FEAT // K_PASS
 GW = 2 * FEAT // K_PASS
 NT = 512
-HALF = 1024
+WQ_PIECES = (
+    (0, 0, 512), (1, 0, 512), (2, 0, 512), (3, 0, 512),
+    (0, 512, 1024), (1, 512, 1024), (2, 512, 1536), (3, 512, 2048),
+    (0, 1024, 2048), (1, 1024, 2048), (2, 1536, 2048),
+)
+ACC2_BANK = (4, 5, 2, 3, 6)
 SPLIT = (512, 1024, 1024, 1536, 1536, 1792, 1792, 1792)
 GROUPS = ((0, 512), (512, 1024), (1024, 1536), (1536, 1792), (1792, 2048))
 SLOPE = 0.01
@@ -97,12 +102,11 @@ def tile_pinsageconv_w_kernel(tc, h_node, h_ngbrs, alpha, Wq_words, Wq_scales, b
                 out=wq_pl[32 * q : 32 * q + 16, :].bitcast(I32),
                 in_=Wq_scales[:, 4 * q : 4 * q + 4, :].bitcast(I32),
             )
-        for h in range(2):
-            for g in range(GQ):
-                nc.sync.dma_start(
-                    out=wq[:, g, h * HALF : (h + 1) * HALF],
-                    in_=Wq_words[g, :, h * HALF : (h + 1) * HALF, :].rearrange("p n t -> p (n t)").bitcast(I32),
-                )
+        for g, lo, hi in WQ_PIECES:
+            nc.sync.dma_start(
+                out=wq[:, g, lo:hi],
+                in_=Wq_words[g, :, lo:hi, :].rearrange("p n t -> p (n t)").bitcast(I32),
+            )
         nc.sync.dma_start(out=xh[:], in_=h_node)
         for hh in range(2):
             for q in (0, 2, 1, 3):
@@ -174,88 +178,61 @@ def tile_pinsageconv_w_kernel(tc, h_node, h_ngbrs, alpha, Wq_words, Wq_scales, b
             bias_evac(4 + j, pbs2[j])
 
         acc1 = {}
-        for h in range(2):
+        for j in range(4):
             for kk in range(NB):
-                for cc in range(2):
-                    acc1[(h, kk, cc)] = bank(4 * h + 2 * kk + cc, [P, NT], F32, "acc1_%d%d%d" % (h, kk, cc))
-            for g in range(GQ):
+                acc1[(j, kk)] = bank(2 * j + kk, [P, NT], F32, "acc1_%d%d" % (j, kk))
+        seen1 = [0] * 4
+        for g, lo, hi in WQ_PIECES:
+            for j in range(lo // NT, hi // NT):
                 for kk in range(NB):
                     unit = kk * GQ + g
-                    for cc in range(2):
-                        c0 = h * HALF + cc * NT
-                        nc.tensor.matmul_mx(
-                            out=acc1[(h, kk, cc)][:],
-                            lhsT=cx[:, unit * P : (unit + 1) * P].bitcast(FP8X4),
-                            lhsT_scale=px[:, unit * P : (unit + 1) * P],
-                            rhs=wq[:, g, c0 : c0 + NT].bitcast(FP8X4),
-                            rhs_scale=wq_pl[4 * g : P, c0 : c0 + NT],
-                            start=(g == 0),
-                            stop=(g == GQ - 1),
-                        )
-
-        def add_bias1(h, kk, v):
-            for cc in range(2):
-                c0 = h * HALF + cc * NT
-                nc.vector.tensor_tensor(out=v[:, cc * NT : (cc + 1) * NT], in0=acc1[(h, kk, cc)][:], in1=bias_b[:, c0 : c0 + NT], op=ALU.add)
+                    nc.tensor.matmul_mx(
+                        out=acc1[(j, kk)][:],
+                        lhsT=cx[:, unit * P : (unit + 1) * P].bitcast(FP8X4),
+                        lhsT_scale=px[:, unit * P : (unit + 1) * P],
+                        rhs=wq[:, g, j * NT : (j + 1) * NT].bitcast(FP8X4),
+                        rhs_scale=wq_pl[4 * g : P, j * NT : (j + 1) * NT],
+                        start=(seen1[j] == 0),
+                        stop=(seen1[j] == GQ - 1),
+                    )
+                seen1[j] += 1
 
         def lrelu(dst, v):
             nc.vector.scalar_tensor_tensor(out=dst, in0=v, scalar=SLOPE, in1=v, op0=ALU.mult, op1=ALU.max)
 
-        def agg_transposes(gp, b):
-            pt = bank(b, [P, 4, P], BF16, "ta%d" % gp)
+        vs, us, ys = {}, {}, {}
+
+        def e_add(j):
+            vs[j] = work.tile([P, NB, NT], F32, tag="v", name="v%d" % j)
+            for kk in range(NB):
+                nc.vector.tensor_tensor(out=vs[j][:, kk, :], in0=acc1[(j, kk)][:], in1=bias_b[:, j * NT : (j + 1) * NT], op=ALU.add)
+
+        def e_lrelu_mul(j):
+            us[j] = work.tile([P, NB, NT], F32, tag="u", name="u%d" % j)
+            ys[j] = work.tile([P, NT], F32, tag="y", name="y%d" % j)
+            lrelu(us[j][:].rearrange("p k n -> p (k n)"), vs[j][:].rearrange("p k n -> p (k n)"))
+            nc.scalar.activation(out=ys[j][:], in_=us[j][:, 0, :], func=ACT.Copy, scale=wgt[:, 0:1])
+
+        def e_fma_transpose(j):
+            nc.vector.scalar_tensor_tensor(out=hagg[:, j * NT : (j + 1) * NT], in0=us[j][:, 1, :], scalar=wgt[:, 1:2], in1=ys[j][:], op0=ALU.mult, op1=ALU.add)
+            pt = bank(j % 2, [P, 4, P], BF16, "ta%d" % j)
             for t in range(4):
-                nc.tensor.transpose(pt[:, t, :], hagg[:, K_PASS * gp + t : K_PASS * (gp + 1) : 4], ident_b[:])
-            return pt
+                nc.tensor.transpose(pt[:, t, :], hagg[:, K_PASS * j + t : K_PASS * (j + 1) : 4], ident_b[:])
+            nc.scalar.copy(out=ga[:, j, :, :], in_=pt[:].rearrange("p t r -> p r t"))
 
-        def agg_evac(eng_copy, gp, pt):
-            eng_copy(out=ga[:, gp, :, :], in_=pt[:].rearrange("p t r -> p r t"))
-
-        v00 = work.tile([P, HALF], F32, tag="v0")
-        u00 = work.tile([P, HALF], F32, tag="u0")
-        v01 = work.tile([P, HALF], F32, tag="v1")
-        u01 = work.tile([P, HALF], F32, tag="u1")
-        y0 = work.tile([P, HALF], F32, tag="y")
-        add_bias1(0, 0, v00)
-        lrelu(u00[:], v00[:])
-        nc.scalar.activation(out=y0[:], in_=u00[:], func=ACT.Copy, scale=wgt[:, 0:1])
-        add_bias1(0, 1, v01)
-        lrelu(u01[:], v01[:])
-        nc.vector.scalar_tensor_tensor(out=hagg[:, 0:HALF], in0=u01[:], scalar=wgt[:, 1:2], in1=y0[:], op0=ALU.mult, op1=ALU.add)
-
-        xhw = xh[:].bitcast(F32)
-        t4 = word_transposes(xhw, 0, 0, "t4")
-        t5 = word_transposes(xhw, 1, 2, "t5")
-        word_evac(nc.scalar.copy, gh, 0, t4)
-        word_evac(nc.scalar.copy, gh, 2, t5)
-
-        v10 = work.tile([P, HALF], F32, tag="v0")
-        u10 = work.tile([P, HALF], F32, tag="u0")
-        v11 = work.tile([P, HALF], F32, tag="v1")
-        u11 = work.tile([P, HALF], F32, tag="u1")
-        y1 = work.tile([P, HALF], F32, tag="y")
-        add_bias1(1, 0, v10)
-        lrelu(u10[:], v10[:])
-        ta0 = agg_transposes(0, 4)
-        ta1 = agg_transposes(1, 5)
-        agg_evac(nc.scalar.copy, 0, ta0)
-        agg_evac(nc.scalar.copy, 1, ta1)
-        nc.scalar.activation(out=y1[:], in_=u10[:], func=ACT.Copy, scale=wgt[:, 0:1])
-        quantise(gh, ch, ph, 0, 4)
-        add_bias1(1, 1, v11)
-        quantise(ga, ca, pa, 0, 2)
-        lrelu(u11[:], v11[:])
-        nc.vector.scalar_tensor_tensor(out=hagg[:, HALF:FEAT], in0=u11[:], scalar=wgt[:, 1:2], in1=y1[:], op0=ALU.mult, op1=ALU.add)
-
-        acc2 = [bank(j, [P, hi - lo], F32, "acc2_%d" % j) for j, (lo, hi) in enumerate(GROUPS)]
         todo = []
         for g, lo, hi in pieces:
             for j, (glo, ghi) in enumerate(GROUPS):
                 if lo <= glo and ghi <= hi:
                     todo.append((g, j))
+        node_first = len([1 for g, lo, hi in pieces[:GQ] for glo, ghi in GROUPS if lo <= glo and ghi <= hi])
+        acc2 = {}
         seen = [0] * len(GROUPS)
 
         def pass2(g, j):
             lo, hi = GROUPS[j]
+            if j not in acc2:
+                acc2[j] = bank(ACC2_BANK[j], [P, hi - lo], F32, "acc2_%d" % j)
             if g < GQ:
                 codes, plane, unit = ch, ph, g
             else:
@@ -271,14 +248,31 @@ def tile_pinsageconv_w_kernel(tc, h_node, h_ngbrs, alpha, Wq_words, Wq_scales, b
             )
             seen[j] += 1
 
-        for g, j in todo[:3]:
+        e_add(0)
+        e_lrelu_mul(0)
+        e_add(1)
+        e_fma_transpose(0)
+        e_lrelu_mul(1)
+        xhw = xh[:].bitcast(F32)
+        t4 = word_transposes(xhw, 2, 0, "t4")
+        t5 = word_transposes(xhw, 3, 2, "t5")
+        word_evac(nc.scalar.copy, gh, 0, t4)
+        word_evac(nc.scalar.copy, gh, 2, t5)
+        e_add(2)
+        e_fma_transpose(1)
+        quantise(ga, ca, pa, 0, 1)
+        e_lrelu_mul(2)
+        quantise(gh, ch, ph, 0, 4)
+        for g, j in todo[:node_first]:
             pass2(g, j)
-        ta2 = agg_transposes(2, 6)
-        ta3 = agg_transposes(3, 7)
-        agg_evac(nc.scalar.copy, 2, ta2)
-        agg_evac(nc.vector.tensor_copy, 3, ta3)
-        quantise(ga, ca, pa, 2, 2)
-        for g, j in todo[3:]:
+        e_add(3)
+        e_fma_transpose(2)
+        quantise(ga, ca, pa, 1, 1)
+        e_lrelu_mul(3)
+        quantise(ga, ca, pa, 2, 1)
+        e_fma_transpose(3)
+        quantise(ga, ca, pa, 3, 1)
+        for g, j in todo[node_first:]:
             pass2(g, j)
 
         junk = keep.tile([P, NT], F32)

@@ -66,7 +66,7 @@ def tile_pinsageconv_w_kernel(tc, h_node, h_ngbrs, alpha, Wq_words, Wq_scales, b
         ident_f = keep.tile([P, P], F32)
         ident_b = keep.tile([P, P], BF16)
         brow = keep.tile([P, NT], BF16)
-        bias_b = keep.tile([P, 2 * FEAT], F32)
+        bias_b = keep.tile([P, 2 * FEAT], BF16)
         a_bf = keep.tile([P, NB], BF16)
         a_f = keep.tile([P, NB], F32)
         a_sum = keep.tile([P, 1], F32)
@@ -95,8 +95,9 @@ def tile_pinsageconv_w_kernel(tc, h_node, h_ngbrs, alpha, Wq_words, Wq_scales, b
         nc.scalar.dma_start(out=a_bf[:], in_=alpha.rearrange("n k o -> n (k o)"))
         nc.scalar.activation(out=warm[:], in_=one[:], func=ACT.Abs_reciprocal_sqrt)
 
-        for kk in range(NB):
-            nc.sync.dma_start(out=xn[:, kk, :], in_=h_ngbrs[:, kk, :])
+        for hf in range(2):
+            half = slice(hf * FEAT // 2, (hf + 1) * FEAT // 2)
+            nc.sync.dma_start(out=xn[:, :, half], in_=h_ngbrs[:, :, half])
         for q in (0, 2, 1, 3):
             nc.sync.dma_start(
                 out=wq_pl[32 * q : 32 * q + 16, :].bitcast(I32),
@@ -122,19 +123,20 @@ def tile_pinsageconv_w_kernel(tc, h_node, h_ngbrs, alpha, Wq_words, Wq_scales, b
             )
 
         def bias_matmul(j, b):
-            pb = bank(b, [P, NT], F32, "pb%d" % j)
-            nc.tensor.matmul(out=pb[:], lhsT=ident_b[:, j : j + 1].to_broadcast([P, P]), rhs=brow[:], start=True, stop=True)
+            pb = bank(b, [P, 2, NT], BF16, "pb%d" % j)
+            for r in range(2):
+                row = 2 * j + r
+                nc.tensor.matmul(out=pb[:, r, :], lhsT=ident_b[:, row : row + 1].to_broadcast([P, P]), rhs=brow[:], start=True, stop=True)
             return pb
 
         def bias_evac(j, pb):
-            nc.scalar.copy(out=bias_b[:, j * NT : (j + 1) * NT], in_=pb[:])
+            nc.scalar.copy(out=bias_b[:, 2 * j * NT : 2 * (j + 1) * NT], in_=pb[:].rearrange("p r n -> p (r n)"))
 
-        def word_transposes(src_words, b, unit0, name):
+        def word_transposes(src_words, b, bases, name):
             pt = bank(b, [P, 2, 2, P], F32, name)
             for a in range(2):
-                base = 256 * (unit0 + a)
                 for u in range(2):
-                    nc.tensor.transpose(pt[:, a, u, :], src_words[:, base + u : base + 256 : 2], ident_f[:])
+                    nc.tensor.transpose(pt[:, a, u, :], src_words[:, bases[a] + u : bases[a] + 256 : 2], ident_f[:])
             return pt
 
         def word_evac(eng_copy, dst, unit0, pt):
@@ -150,32 +152,20 @@ def tile_pinsageconv_w_kernel(tc, h_node, h_ngbrs, alpha, Wq_words, Wq_scales, b
                 in_=src[:, unit0 : unit0 + units, :, :].rearrange("p a r t -> p (a r t)"),
             )
 
-        pbs = [bias_matmul(j, 4 + j) for j in range(4)]
-        bias_evac(0, pbs[0])
-        bias_evac(1, pbs[1])
         xnw = xn[:].rearrange("p k f -> p (k f)").bitcast(F32)
-        t0 = word_transposes(xnw, 0, 0, "t0")
-        t1 = word_transposes(xnw, 1, 2, "t1")
-        word_evac(nc.vector.tensor_copy, gx, 0, t0)
-        word_evac(nc.scalar.copy, gx, 2, t1)
-        bias_evac(2, pbs[2])
-        bias_evac(3, pbs[3])
-        t2 = word_transposes(xnw, 2, 4, "t2")
-        t3 = word_transposes(xnw, 3, 6, "t3")
-        word_evac(nc.vector.tensor_copy, gx, 4, t2)
-        word_evac(nc.scalar.copy, gx, 6, t3)
-        quantise(gx, cx, px, 0, 4)
-        quantise(gx, cx, px, 4, 4)
+        for g in range(GQ):
+            tx = word_transposes(xnw, g, [kk * FEAT // 2 + 256 * g for kk in range(NB)], "tx%d" % g)
+            word_evac(nc.vector.tensor_copy if g % 2 == 0 else nc.scalar.copy, gx, NB * g, tx)
+            quantise(gx, cx, px, NB * g, NB)
+        pbs = [bias_matmul(j, 4 + j) for j in range(4)]
+        for j in range(4):
+            bias_evac(j, pbs[j])
 
         nc.vector.tensor_copy(out=a_f[:], in_=a_bf[:])
         nc.vector.tensor_tensor(out=a_sum[:], in0=a_f[:, 0:1], in1=a_f[:, 1:2], op=ALU.add)
         nc.vector.scalar_tensor_tensor(out=a_safe[:], in0=a_sum[:], scalar=0.0, in1=a_sum[:], op0=ALU.is_equal, op1=ALU.add)
         nc.vector.reciprocal(out=a_rec[:], in_=a_safe[:])
         nc.vector.tensor_scalar(out=wgt[:], in0=a_f[:], scalar1=a_rec[:, 0:1], scalar2=None, op0=ALU.mult)
-
-        pbs2 = [bias_matmul(4 + j, 4 + j) for j in range(4)]
-        for j in range(4):
-            bias_evac(4 + j, pbs2[j])
 
         acc1 = {}
         for j in range(4):
@@ -185,7 +175,7 @@ def tile_pinsageconv_w_kernel(tc, h_node, h_ngbrs, alpha, Wq_words, Wq_scales, b
         for g, lo, hi in WQ_PIECES:
             for j in range(lo // NT, hi // NT):
                 for kk in range(NB):
-                    unit = kk * GQ + g
+                    unit = NB * g + kk
                     nc.tensor.matmul_mx(
                         out=acc1[(j, kk)][:],
                         lhsT=cx[:, unit * P : (unit + 1) * P].bitcast(FP8X4),
@@ -254,8 +244,8 @@ def tile_pinsageconv_w_kernel(tc, h_node, h_ngbrs, alpha, Wq_words, Wq_scales, b
         e_fma_transpose(0)
         e_lrelu_mul(1)
         xhw = xh[:].bitcast(F32)
-        t4 = word_transposes(xhw, 2, 0, "t4")
-        t5 = word_transposes(xhw, 3, 2, "t5")
+        t4 = word_transposes(xhw, 2, (0, 256), "t4")
+        t5 = word_transposes(xhw, 3, (512, 768), "t5")
         word_evac(nc.scalar.copy, gh, 0, t4)
         word_evac(nc.scalar.copy, gh, 2, t5)
         e_add(2)

@@ -27,7 +27,7 @@ WQ_PIECES = (
     (0, 1024, 2048), (1, 1024, 2048), (2, 1536, 2048),
 )
 ACC2_BANK = (4, 5, 2, 3, 6)
-SPLIT = (512, 1024, 1024, 1536, 1536, 1792, 1792, 1792)
+SPLIT = (512, 1024, 1536, 1792, 1792, 1792, 1792, 1792)
 GROUPS = ((0, 512), (512, 1024), (1024, 1536), (1536, 1792), (1792, 2048))
 SLOPE = 0.01
 TINY = 1e-30
@@ -78,20 +78,24 @@ def tile_pinsageconv_w_kernel(tc, h_node, h_ngbrs, alpha, Wq_words, Wq_scales, b
         hagg = keep.tile([P, FEAT], BF16)
         h2 = keep.tile([P, FEAT], F32)
         res = keep.tile([P, FEAT], F32)
-        ssp = keep.tile([P, 5], F32)
+        ssp = keep.tile([P, 4], F32)
+        sq_all = keep.tile([P, 1], F32)
+        sq_pos = keep.tile([P, 1], F32)
+        ss_rest = keep.tile([P, 1], F32)
+        junk_v = keep.tile([P, 256], F32)
         ss01 = keep.tile([P, 1], F32)
         ssprev = keep.tile([P, 1], F32)
         rn = keep.tile([P, 1], F32)
 
-        nc.vector.memset(wq_pl[:].bitcast(I32), 0)
         nc.vector.memset(brow[:], 0.0)
         nc.vector.memset(one[:], 1.0)
+        nc.vector.memset(wq_pl[:].bitcast(I32), 0)
         nc.vector.memset(ww_pl[:].rearrange("p h n -> p (h n)").bitcast(I32), 0)
-        make_identity(nc, ident_f[:])
         make_identity(nc, ident_b[:])
+        make_identity(nc, ident_f[:])
 
-        nc.scalar.dma_start(out=brow[0:4, :], in_=bq.rearrange("(c n) -> c n", c=4))
-        nc.scalar.dma_start(out=brow[4:8, :], in_=bw.rearrange("(c n) -> c n", c=4))
+        nc.sync.dma_start(out=brow[0:4, :], in_=bq.rearrange("(c n) -> c n", c=4))
+        nc.sync.dma_start(out=brow[4:8, :], in_=bw.rearrange("(c n) -> c n", c=4))
         nc.scalar.dma_start(out=a_bf[:], in_=alpha.rearrange("n k o -> n (k o)"))
         nc.scalar.activation(out=warm[:], in_=one[:], func=ACT.Abs_reciprocal_sqrt)
 
@@ -109,14 +113,18 @@ def tile_pinsageconv_w_kernel(tc, h_node, h_ngbrs, alpha, Wq_words, Wq_scales, b
                 in_=Wq_words[g, :, lo:hi, :].rearrange("p n t -> p (n t)").bitcast(I32),
             )
         nc.sync.dma_start(out=xh[:], in_=h_node)
-        for hh in range(2):
+        pieces = [(g, 0, SPLIT[g]) for g in range(GW)] + [(g, SPLIT[g], FEAT) for g in range(GW)]
+        def ww_plane_loads(hh):
             for q in (0, 2, 1, 3):
                 nc.sync.dma_start(
                     out=ww_pl[32 * q : 32 * q + 16, hh, :].bitcast(I32),
                     in_=Ww_scales[4 * hh : 4 * hh + 4, 4 * q : 4 * q + 4, :].bitcast(I32),
                 )
-        pieces = [(g, 0, SPLIT[g]) for g in range(GW)] + [(g, SPLIT[g], FEAT) for g in range(GW)]
-        for g, lo, hi in pieces:
+
+        ww_plane_loads(0)
+        for n, (g, lo, hi) in enumerate(pieces):
+            if n == 3:
+                ww_plane_loads(1)
             nc.sync.dma_start(
                 out=ww[:, g, lo:hi],
                 in_=Ww_words[g, :, lo:hi, :].rearrange("p n t -> p (n t)").bitcast(I32),
@@ -152,15 +160,14 @@ def tile_pinsageconv_w_kernel(tc, h_node, h_ngbrs, alpha, Wq_words, Wq_scales, b
                 in_=src[:, unit0 : unit0 + units, :, :].rearrange("p a r t -> p (a r t)"),
             )
 
+        pbs = [bias_matmul(j, 4 + j) for j in range(2)]
+        for j in range(2):
+            bias_evac(j, pbs[j])
         xnw = xn[:].rearrange("p k f -> p (k f)").bitcast(F32)
         for g in range(GQ):
             tx = word_transposes(xnw, g, [kk * FEAT // 2 + 256 * g for kk in range(NB)], "tx%d" % g)
             word_evac(nc.vector.tensor_copy if g % 2 == 0 else nc.scalar.copy, gx, NB * g, tx)
             quantise(gx, cx, px, NB * g, NB)
-        pbs = [bias_matmul(j, 4 + j) for j in range(4)]
-        for j in range(4):
-            bias_evac(j, pbs[j])
-
         nc.vector.tensor_copy(out=a_f[:], in_=a_bf[:])
         nc.vector.tensor_tensor(out=a_sum[:], in0=a_f[:, 0:1], in1=a_f[:, 1:2], op=ALU.add)
         nc.vector.scalar_tensor_tensor(out=a_safe[:], in0=a_sum[:], scalar=0.0, in1=a_sum[:], op0=ALU.is_equal, op1=ALU.add)
@@ -210,12 +217,6 @@ def tile_pinsageconv_w_kernel(tc, h_node, h_ngbrs, alpha, Wq_words, Wq_scales, b
                 nc.tensor.transpose(pt[:, t, :], hagg[:, K_PASS * j + t : K_PASS * (j + 1) : 4], ident_b[:])
             nc.scalar.copy(out=ga[:, j, :, :], in_=pt[:].rearrange("p t r -> p r t"))
 
-        todo = []
-        for g, lo, hi in pieces:
-            for j, (glo, ghi) in enumerate(GROUPS):
-                if lo <= glo and ghi <= hi:
-                    todo.append((g, j))
-        node_first = len([1 for g, lo, hi in pieces[:GQ] for glo, ghi in GROUPS if lo <= glo and ghi <= hi])
         acc2 = {}
         seen = [0] * len(GROUPS)
 
@@ -238,48 +239,63 @@ def tile_pinsageconv_w_kernel(tc, h_node, h_ngbrs, alpha, Wq_words, Wq_scales, b
             )
             seen[j] += 1
 
+        def passes(first, end):
+            for g, lo, hi in pieces[first:end]:
+                for j, (glo, ghi) in enumerate(GROUPS):
+                    if lo <= glo and ghi <= hi:
+                        pass2(g, j)
+
         e_add(0)
         e_lrelu_mul(0)
+        bias_evac(2, bias_matmul(2, 1))
         e_add(1)
         e_fma_transpose(0)
-        e_lrelu_mul(1)
         xhw = xh[:].bitcast(F32)
         t4 = word_transposes(xhw, 2, (0, 256), "t4")
         t5 = word_transposes(xhw, 3, (512, 768), "t5")
         word_evac(nc.scalar.copy, gh, 0, t4)
         word_evac(nc.scalar.copy, gh, 2, t5)
+        e_lrelu_mul(1)
         e_add(2)
-        e_fma_transpose(1)
-        quantise(ga, ca, pa, 0, 1)
-        e_lrelu_mul(2)
         quantise(gh, ch, ph, 0, 4)
-        for g, j in todo[:node_first]:
-            pass2(g, j)
+        e_fma_transpose(1)
+        passes(0, GQ)
+        e_lrelu_mul(2)
+        quantise(ga, ca, pa, 0, 1)
         e_add(3)
+        bias_evac(3, bias_matmul(3, 7))
         e_fma_transpose(2)
         quantise(ga, ca, pa, 1, 1)
+        passes(GQ, GQ + 1)
         e_lrelu_mul(3)
         quantise(ga, ca, pa, 2, 1)
         e_fma_transpose(3)
+        passes(GQ + 1, GQ + 2)
         quantise(ga, ca, pa, 3, 1)
-        for g, j in todo[node_first:]:
-            pass2(g, j)
+        passes(GQ + 2, len(pieces))
 
         junk = keep.tile([P, NT], F32)
 
-        def epilogue2(j):
+        def add2(j):
             lo, hi = GROUPS[j]
-            v = work.tile([P, NT], F32, tag="v2")
+            v = work.tile([P, NT], F32, tag="v2", name="v2_%d" % j)
             nc.vector.tensor_tensor(out=v[:, 0 : hi - lo], in0=acc2[j][:], in1=bias_b[:, FEAT + lo : FEAT + hi], op=ALU.add)
-            lrelu(h2[:, lo:hi], v[:, 0 : hi - lo])
-            nc.scalar.activation(out=junk[:, 0 : hi - lo], in_=h2[:, lo:hi], func=ACT.Square, accum_out=ssp[:, j : j + 1])
+            return v[:, 0 : hi - lo]
 
         for j in range(4):
-            epilogue2(j)
-        epilogue2(4)
-        nc.vector.tensor_reduce(out=ss01[:], in_=ssp[:, 0:4], op=ALU.add, axis=mybir.AxisListType.X)
+            lo, hi = GROUPS[j]
+            lrelu(h2[:, lo:hi], add2(j))
+            nc.scalar.activation(out=junk[:, 0 : hi - lo], in_=h2[:, lo:hi], func=ACT.Square, accum_out=ssp[:, j : j + 1])
+
+        lo, hi = GROUPS[4]
+        v4 = add2(4)
+        nc.scalar.activation(out=junk[:, 0 : hi - lo], in_=v4, func=ACT.Square, scale=SLOPE, accum_out=sq_all[:])
+        nc.vector.scalar_tensor_tensor(out=junk_v[:], in0=v4, scalar=0.0, in1=v4, op0=ALU.max, op1=ALU.mult, accum_out=sq_pos[:])
+        nc.vector.tensor_reduce(out=ss01[:], in_=ssp[:], op=ALU.add, axis=mybir.AxisListType.X)
         nc.vector.tensor_scalar(out=ssprev[:], in0=ss01[:], scalar1=TINY, scalar2=None, op0=ALU.add)
-        nc.scalar.activation(out=rn[:], in_=ssp[:, 4:5], func=ACT.Abs_reciprocal_sqrt, bias=ssprev[:, 0:1], scale=1.0)
+        nc.vector.scalar_tensor_tensor(out=ss_rest[:], in0=sq_pos[:], scalar=1.0 - SLOPE * SLOPE, in1=ssprev[:], op0=ALU.mult, op1=ALU.add)
+        nc.scalar.activation(out=rn[:], in_=sq_all[:], func=ACT.Abs_reciprocal_sqrt, bias=ss_rest[:, 0:1], scale=1.0)
+        lrelu(h2[:, lo:hi], v4)
 
         def scale_v(c):
             cols = slice(c * NT, (c + 1) * NT)

@@ -94,8 +94,8 @@ def tile_pinsageconv_w_kernel(tc, h_node, h_ngbrs, alpha, Wq_words, Wq_scales, b
         make_identity(nc, ident_b[:])
         make_identity(nc, ident_f[:])
 
-        nc.sync.dma_start(out=brow[0:4, :], in_=bq.rearrange("(c n) -> c n", c=4))
-        nc.sync.dma_start(out=brow[4:8, :], in_=bw.rearrange("(c n) -> c n", c=4))
+        nc.scalar.dma_start(out=brow[0:4, :], in_=bq.rearrange("(c n) -> c n", c=4))
+        nc.scalar.dma_start(out=brow[4:8, :], in_=bw.rearrange("(c n) -> c n", c=4))
         nc.scalar.dma_start(out=a_bf[:], in_=alpha.rearrange("n k o -> n (k o)"))
         nc.scalar.activation(out=warm[:], in_=one[:], func=ACT.Abs_reciprocal_sqrt)
 
@@ -113,18 +113,14 @@ def tile_pinsageconv_w_kernel(tc, h_node, h_ngbrs, alpha, Wq_words, Wq_scales, b
                 in_=Wq_words[g, :, lo:hi, :].rearrange("p n t -> p (n t)").bitcast(I32),
             )
         nc.sync.dma_start(out=xh[:], in_=h_node)
-        pieces = [(g, 0, SPLIT[g]) for g in range(GW)] + [(g, SPLIT[g], FEAT) for g in range(GW)]
-        def ww_plane_loads(hh):
+        for hh in range(2):
             for q in (0, 2, 1, 3):
                 nc.sync.dma_start(
                     out=ww_pl[32 * q : 32 * q + 16, hh, :].bitcast(I32),
                     in_=Ww_scales[4 * hh : 4 * hh + 4, 4 * q : 4 * q + 4, :].bitcast(I32),
                 )
-
-        ww_plane_loads(0)
-        for n, (g, lo, hi) in enumerate(pieces):
-            if n == 3:
-                ww_plane_loads(1)
+        pieces = [(g, 0, SPLIT[g]) for g in range(GW)] + [(g, SPLIT[g], FEAT) for g in range(GW)]
+        for g, lo, hi in pieces:
             nc.sync.dma_start(
                 out=ww[:, g, lo:hi],
                 in_=Ww_words[g, :, lo:hi, :].rearrange("p n t -> p (n t)").bitcast(I32),

@@ -21,17 +21,12 @@ K_PASS = 512
 GQ = FEAT // K_PASS
 GW = 2 * FEAT // K_PASS
 NT = 512
-WQ_PIECES = (
-    (0, 0, 512), (1, 0, 512), (2, 0, 512), (3, 0, 512),
-    (0, 512, 1024), (1, 512, 1024), (2, 512, 1536), (3, 512, 2048),
-    (0, 1024, 2048), (1, 1024, 2048), (2, 1536, 2048),
-)
+WQ_CUTS = (0, 512, 1024, 2048)
 ACC2_BANK = (4, 5, 2, 3, 6)
-SPLIT = (512, 1024, 1536, 1792, 1792, 1792, 1792, 1792)
 GROUPS = ((0, 512), (512, 1024), (1024, 1536), (1536, 1792), (1792, 2048))
+LAST = GROUPS[4][0]
 SLOPE = 0.01
 TINY = 1e-30
-PIN = False
 
 FLOPS = 2 * P * NB * FEAT * FEAT + 2 * P * 2 * FEAT * FEAT
 
@@ -39,8 +34,7 @@ FLOPS = 2 * P * NB * FEAT * FEAT + 2 * P * 2 * FEAT * FEAT
 def tile_pinsageconv_w_kernel(tc, h_node, h_ngbrs, alpha, Wq_words, Wq_scales, bq, Ww_words, Ww_scales, bw, out):
     nc = tc.nc
     with ExitStack() as ctx:
-        if PIN:
-            ctx.enter_context(tc.manual_schedule())
+        ctx.enter_context(tc.manual_schedule(engines={mybir.EngineType.PE}))
         keep = ctx.enter_context(tc.tile_pool(name="keep", bufs=1))
         work = ctx.enter_context(tc.tile_pool(name="work", bufs=2))
         psum = ctx.enter_context(tc.psum_pool(name="psum", bufs=1))
@@ -107,23 +101,27 @@ def tile_pinsageconv_w_kernel(tc, h_node, h_ngbrs, alpha, Wq_words, Wq_scales, b
                 out=wq_pl[32 * q : 32 * q + 16, :].bitcast(I32),
                 in_=Wq_scales[:, 4 * q : 4 * q + 4, :].bitcast(I32),
             )
-        for g, lo, hi in WQ_PIECES:
-            nc.sync.dma_start(
-                out=wq[:, g, lo:hi],
-                in_=Wq_words[g, :, lo:hi, :].rearrange("p n t -> p (n t)").bitcast(I32),
-            )
-        nc.sync.dma_start(out=xh[:], in_=h_node)
+        for lo, hi in zip(WQ_CUTS, WQ_CUTS[1:]):
+            if lo == WQ_CUTS[2]:
+                nc.sync.dma_start(out=xh[:], in_=h_node)
+            for g in range(GQ):
+                nc.sync.dma_start(
+                    out=wq[:, g, lo:hi],
+                    in_=Wq_words[g, :, lo:hi, :].rearrange("p n t -> p (n t)").bitcast(I32),
+                )
         for hh in range(2):
             for q in (0, 2, 1, 3):
                 nc.sync.dma_start(
                     out=ww_pl[32 * q : 32 * q + 16, hh, :].bitcast(I32),
                     in_=Ww_scales[4 * hh : 4 * hh + 4, 4 * q : 4 * q + 4, :].bitcast(I32),
                 )
-        pieces = [(g, 0, SPLIT[g]) for g in range(GW)] + [(g, SPLIT[g], FEAT) for g in range(GW)]
-        for g, lo, hi in pieces:
+        pieces = [(g, g + 1, 0, LAST) for g in range(GQ)]
+        pieces += [(g, g + 2, lo, hi) for lo, hi in GROUPS[:4] for g in (4, 6)]
+        pieces += [(g0, g1, LAST, FEAT) for g0, g1 in ((0, 4), (4, 6), (6, 7), (7, 8))]
+        for g0, g1, lo, hi in pieces:
             nc.sync.dma_start(
-                out=ww[:, g, lo:hi],
-                in_=Ww_words[g, :, lo:hi, :].rearrange("p n t -> p (n t)").bitcast(I32),
+                out=ww[:, g0:g1, lo:hi],
+                in_=Ww_words[g0:g1, :, lo:hi, :].rearrange("g p n t -> p g (n t)").bitcast(I32),
             )
 
         def bias_matmul(j, b):
@@ -156,9 +154,6 @@ def tile_pinsageconv_w_kernel(tc, h_node, h_ngbrs, alpha, Wq_words, Wq_scales, b
                 in_=src[:, unit0 : unit0 + units, :, :].rearrange("p a r t -> p (a r t)"),
             )
 
-        pbs = [bias_matmul(j, 4 + j) for j in range(2)]
-        for j in range(2):
-            bias_evac(j, pbs[j])
         xnw = xn[:].rearrange("p k f -> p (k f)").bitcast(F32)
         for g in range(GQ):
             tx = word_transposes(xnw, g, [kk * FEAT // 2 + 256 * g for kk in range(NB)], "tx%d" % g)
@@ -171,24 +166,25 @@ def tile_pinsageconv_w_kernel(tc, h_node, h_ngbrs, alpha, Wq_words, Wq_scales, b
         nc.vector.tensor_scalar(out=wgt[:], in0=a_f[:], scalar1=a_rec[:, 0:1], scalar2=None, op0=ALU.mult)
 
         acc1 = {}
-        for j in range(4):
-            for kk in range(NB):
-                acc1[(j, kk)] = bank(2 * j + kk, [P, NT], F32, "acc1_%d%d" % (j, kk))
-        seen1 = [0] * 4
-        for g, lo, hi in WQ_PIECES:
-            for j in range(lo // NT, hi // NT):
+
+        def passes1(lo, hi):
+            js = range(lo // NT, hi // NT)
+            for j in js:
                 for kk in range(NB):
-                    unit = NB * g + kk
-                    nc.tensor.matmul_mx(
-                        out=acc1[(j, kk)][:],
-                        lhsT=cx[:, unit * P : (unit + 1) * P].bitcast(FP8X4),
-                        lhsT_scale=px[:, unit * P : (unit + 1) * P],
-                        rhs=wq[:, g, j * NT : (j + 1) * NT].bitcast(FP8X4),
-                        rhs_scale=wq_pl[4 * g : P, j * NT : (j + 1) * NT],
-                        start=(seen1[j] == 0),
-                        stop=(seen1[j] == GQ - 1),
-                    )
-                seen1[j] += 1
+                    acc1[(j, kk)] = bank(2 * j + kk, [P, NT], F32, "acc1_%d%d" % (j, kk))
+            for j in js:
+                for g in range(GQ):
+                    for kk in range(NB):
+                        unit = NB * g + kk
+                        nc.tensor.matmul_mx(
+                            out=acc1[(j, kk)][:],
+                            lhsT=cx[:, unit * P : (unit + 1) * P].bitcast(FP8X4),
+                            lhsT_scale=px[:, unit * P : (unit + 1) * P],
+                            rhs=wq[:, g, j * NT : (j + 1) * NT].bitcast(FP8X4),
+                            rhs_scale=wq_pl[4 * g : P, j * NT : (j + 1) * NT],
+                            start=(g == 0),
+                            stop=(g == GQ - 1),
+                        )
 
         def lrelu(dst, v):
             nc.vector.scalar_tensor_tensor(out=dst, in0=v, scalar=SLOPE, in1=v, op0=ALU.mult, op1=ALU.max)
@@ -236,39 +232,46 @@ def tile_pinsageconv_w_kernel(tc, h_node, h_ngbrs, alpha, Wq_words, Wq_scales, b
             seen[j] += 1
 
         def passes(first, end):
-            for g, lo, hi in pieces[first:end]:
-                for j, (glo, ghi) in enumerate(GROUPS):
-                    if lo <= glo and ghi <= hi:
-                        pass2(g, j)
+            for g0, g1, lo, hi in pieces[first:end]:
+                for g in range(g0, g1):
+                    for j, (glo, ghi) in enumerate(GROUPS):
+                        if lo <= glo and ghi <= hi:
+                            pass2(g, j)
 
+        bias_evac(0, bias_matmul(0, 4))
+        passes1(0, 512)
+        bias_evac(1, bias_matmul(1, 5))
+        passes1(512, 1024)
+        for j in range(2, 4):
+            bias_evac(j, bias_matmul(j, 4 + j))
         e_add(0)
         e_lrelu_mul(0)
-        bias_evac(2, bias_matmul(2, 1))
-        e_add(1)
-        e_fma_transpose(0)
         xhw = xh[:].bitcast(F32)
-        t4 = word_transposes(xhw, 2, (0, 256), "t4")
-        t5 = word_transposes(xhw, 3, (512, 768), "t5")
+        t4 = word_transposes(xhw, 0, (0, 256), "t4")
+        t5 = word_transposes(xhw, 1, (512, 768), "t5")
         word_evac(nc.scalar.copy, gh, 0, t4)
         word_evac(nc.scalar.copy, gh, 2, t5)
+        passes1(1024, 1536)
+        e_add(1)
+        e_fma_transpose(0)
+        passes1(1536, 2048)
         e_lrelu_mul(1)
-        e_add(2)
         quantise(gh, ch, ph, 0, 4)
+        e_add(2)
         e_fma_transpose(1)
-        passes(0, GQ)
-        e_lrelu_mul(2)
         quantise(ga, ca, pa, 0, 1)
+        passes(0, 2)
+        e_lrelu_mul(2)
         e_add(3)
-        bias_evac(3, bias_matmul(3, 7))
-        e_fma_transpose(2)
         quantise(ga, ca, pa, 1, 1)
-        passes(GQ, GQ + 1)
+        e_fma_transpose(2)
+        passes(2, 3)
         e_lrelu_mul(3)
         quantise(ga, ca, pa, 2, 1)
         e_fma_transpose(3)
-        passes(GQ + 1, GQ + 2)
+        passes(3, 4)
         quantise(ga, ca, pa, 3, 1)
-        passes(GQ + 2, len(pieces))
+        passes(4, len(pieces))
 
         junk = keep.tile([P, NT], F32)
 

@@ -24,7 +24,6 @@ NT = 512
 WQ_CUTS = (0, 512, 1024, 2048)
 ACC2_BANK = (4, 5, 2, 3, 6)
 GROUPS = ((0, 512), (512, 1024), (1024, 1536), (1536, 1792), (1792, 2048))
-LAST = GROUPS[4][0]
 SLOPE = 0.01
 TINY = 1e-30
 
@@ -60,6 +59,7 @@ def tile_pinsageconv_w_kernel(tc, h_node, h_ngbrs, alpha, Wq_words, Wq_scales, b
         ident_f = keep.tile([P, P], F32)
         ident_b = keep.tile([P, P], BF16)
         brow = keep.tile([P, NT], BF16)
+        zeros = keep.tile([P, NT], BF16)
         bias_b = keep.tile([P, 2 * FEAT], BF16)
         a_bf = keep.tile([P, NB], BF16)
         a_f = keep.tile([P, NB], F32)
@@ -76,13 +76,16 @@ def tile_pinsageconv_w_kernel(tc, h_node, h_ngbrs, alpha, Wq_words, Wq_scales, b
         sq_all = keep.tile([P, 1], F32)
         sq_pos = keep.tile([P, 1], F32)
         ss_rest = keep.tile([P, 1], F32)
-        junk_v = keep.tile([P, 256], F32)
-        ss01 = keep.tile([P, 1], F32)
+        junk = keep.tile([P, NT], F32)
+        junk_v = keep.tile([P, NT], F32)
+        v_end = keep.tile([P, NT], F32)
         ssprev = keep.tile([P, 1], F32)
         rn = keep.tile([P, 1], F32)
 
         nc.vector.memset(brow[:], 0.0)
         nc.vector.memset(one[:], 1.0)
+        nc.vector.memset(zeros[:], 0.0)
+        nc.vector.memset(ssp[:, 3:4], TINY)
         nc.vector.memset(wq_pl[:].bitcast(I32), 0)
         nc.vector.memset(ww_pl[:].rearrange("p h n -> p (h n)").bitcast(I32), 0)
         make_identity(nc, ident_b[:])
@@ -109,19 +112,25 @@ def tile_pinsageconv_w_kernel(tc, h_node, h_ngbrs, alpha, Wq_words, Wq_scales, b
                     out=wq[:, g, lo:hi],
                     in_=Wq_words[g, :, lo:hi, :].rearrange("p n t -> p (n t)").bitcast(I32),
                 )
-        for hh in range(2):
-            for q in (0, 2, 1, 3):
-                nc.sync.dma_start(
-                    out=ww_pl[32 * q : 32 * q + 16, hh, :].bitcast(I32),
-                    in_=Ww_scales[4 * hh : 4 * hh + 4, 4 * q : 4 * q + 4, :].bitcast(I32),
-                )
-        pieces = [(g, g + 1, 0, LAST) for g in range(GQ)]
-        pieces += [(g, g + 2, lo, hi) for lo, hi in GROUPS[:4] for g in (4, 6)]
-        pieces += [(g0, g1, LAST, FEAT) for g0, g1 in ((0, 4), (4, 6), (6, 7), (7, 8))]
-        for g0, g1, lo, hi in pieces:
+        for q in (0, 2, 1, 3):
             nc.sync.dma_start(
-                out=ww[:, g0:g1, lo:hi],
-                in_=Ww_words[g0:g1, :, lo:hi, :].rearrange("g p n t -> p g (n t)").bitcast(I32),
+                out=ww_pl[32 * q : 32 * q + 32, 0, :].bitcast(I32),
+                in_=Ww_scales[:, 4 * q : 4 * q + 4, :].bitcast(I32),
+            )
+        pieces = [(g, 0, FEAT) for g in range(4)] + [(4, 0, 1536)]
+        pieces += [(g, lo, hi) for lo, hi in GROUPS[:3] for g in range(5, GW)]
+        pieces += [(4, 1536, FEAT)]
+        pieces += [(g, lo, hi) for lo, hi in GROUPS[3:] for g in range(5, GW)]
+        for n, (g, lo, hi) in enumerate(pieces):
+            if n == 3:
+                for q in (0, 2, 1, 3):
+                    nc.sync.dma_start(
+                        out=ww_pl[32 * q : 32 * q + 16, 1, :].bitcast(I32),
+                        in_=ww_pl[32 * q + 16 : 32 * q + 32, 0, :].bitcast(I32),
+                    )
+            nc.sync.dma_start(
+                out=ww[:, g, lo:hi],
+                in_=Ww_words[g, :, lo:hi, :].rearrange("p n t -> p (n t)").bitcast(I32),
             )
 
         def bias_matmul(j, b):
@@ -153,6 +162,10 @@ def tile_pinsageconv_w_kernel(tc, h_node, h_ngbrs, alpha, Wq_words, Wq_scales, b
                 scales=plane[:, unit0 * P : (unit0 + units) * P],
                 in_=src[:, unit0 : unit0 + units, :, :].rearrange("p a r t -> p (a r t)"),
             )
+
+        idle = bank(7, [P, NT], F32, "idle")
+        for i in range(3):
+            nc.tensor.matmul(out=idle[:], lhsT=ident_b[:], rhs=zeros[:], start=True, stop=True)
 
         xnw = xn[:].rearrange("p k f -> p (k f)").bitcast(F32)
         for g in range(GQ):
@@ -232,11 +245,10 @@ def tile_pinsageconv_w_kernel(tc, h_node, h_ngbrs, alpha, Wq_words, Wq_scales, b
             seen[j] += 1
 
         def passes(first, end):
-            for g0, g1, lo, hi in pieces[first:end]:
-                for g in range(g0, g1):
-                    for j, (glo, ghi) in enumerate(GROUPS):
-                        if lo <= glo and ghi <= hi:
-                            pass2(g, j)
+            for g, lo, hi in pieces[first:end]:
+                for j, (glo, ghi) in enumerate(GROUPS):
+                    if lo <= glo and ghi <= hi:
+                        pass2(g, j)
 
         bias_evac(0, bias_matmul(0, 4))
         passes1(0, 512)
@@ -273,36 +285,32 @@ def tile_pinsageconv_w_kernel(tc, h_node, h_ngbrs, alpha, Wq_words, Wq_scales, b
         quantise(ga, ca, pa, 3, 1)
         passes(4, len(pieces))
 
-        junk = keep.tile([P, NT], F32)
+        ctx.enter_context(tc.manual_schedule())
 
-        def add2(j):
+        def add2(dst, j):
             lo, hi = GROUPS[j]
-            v = work.tile([P, NT], F32, tag="v2", name="v2_%d" % j)
-            nc.vector.tensor_tensor(out=v[:, 0 : hi - lo], in0=acc2[j][:], in1=bias_b[:, FEAT + lo : FEAT + hi], op=ALU.add)
-            return v[:, 0 : hi - lo]
+            nc.vector.tensor_tensor(out=dst, in0=acc2[j][:], in1=bias_b[:, FEAT + lo : FEAT + hi], op=ALU.add)
 
-        for j in range(4):
+        for j in range(3):
             lo, hi = GROUPS[j]
-            lrelu(h2[:, lo:hi], add2(j))
-            nc.scalar.activation(out=junk[:, 0 : hi - lo], in_=h2[:, lo:hi], func=ACT.Square, accum_out=ssp[:, j : j + 1])
+            v = work.tile([P, NT], F32, tag="v2")
+            add2(v[:], j)
+            lrelu(h2[:, lo:hi], v[:])
+            nc.scalar.activation(out=junk[:], in_=h2[:, lo:hi], func=ACT.Square, accum_out=ssp[:, j : j + 1])
 
-        lo, hi = GROUPS[4]
-        v4 = add2(4)
-        nc.scalar.activation(out=junk[:, 0 : hi - lo], in_=v4, func=ACT.Square, scale=SLOPE, accum_out=sq_all[:])
-        nc.vector.scalar_tensor_tensor(out=junk_v[:], in0=v4, scalar=0.0, in1=v4, op0=ALU.max, op1=ALU.mult, accum_out=sq_pos[:])
-        nc.vector.tensor_reduce(out=ss01[:], in_=ssp[:], op=ALU.add, axis=mybir.AxisListType.X)
-        nc.vector.tensor_scalar(out=ssprev[:], in0=ss01[:], scalar1=TINY, scalar2=None, op0=ALU.add)
+        add2(v_end[:, 0:256], 3)
+        add2(v_end[:, 256:512], 4)
+        nc.scalar.activation(out=junk[:], in_=v_end[:], func=ACT.Square, scale=SLOPE, accum_out=sq_all[:])
+        nc.vector.scalar_tensor_tensor(out=junk_v[:], in0=v_end[:], scalar=0.0, in1=v_end[:], op0=ALU.max, op1=ALU.mult, accum_out=sq_pos[:])
+        nc.vector.tensor_reduce(out=ssprev[:], in_=ssp[:], op=ALU.add, axis=mybir.AxisListType.X)
         nc.vector.scalar_tensor_tensor(out=ss_rest[:], in0=sq_pos[:], scalar=1.0 - SLOPE * SLOPE, in1=ssprev[:], op0=ALU.mult, op1=ALU.add)
         nc.scalar.activation(out=rn[:], in_=sq_all[:], func=ACT.Abs_reciprocal_sqrt, bias=ss_rest[:, 0:1], scale=1.0)
-        lrelu(h2[:, lo:hi], v4)
+        lrelu(h2[:, 3 * NT : FEAT], v_end[:])
 
-        def scale_v(c):
+        for c in range(4):
             cols = slice(c * NT, (c + 1) * NT)
-            nc.vector.tensor_scalar(out=res[:, cols], in0=h2[:, cols], scalar1=rn[:, 0:1], scalar2=None, op0=ALU.mult)
+            if c == 2:
+                nc.scalar.activation(out=res[:, cols], in_=h2[:, cols], func=ACT.Copy, scale=rn[:, 0:1])
+            else:
+                nc.vector.tensor_scalar(out=res[:, cols], in0=h2[:, cols], scalar1=rn[:, 0:1], scalar2=None, op0=ALU.mult)
             nc.sync.dma_start(out=out[:, cols], in_=res[:, cols])
-
-        scale_v(0)
-        nc.scalar.activation(out=res[:, 2 * NT : 3 * NT], in_=h2[:, 2 * NT : 3 * NT], func=ACT.Copy, scale=rn[:, 0:1])
-        nc.sync.dma_start(out=out[:, 2 * NT : 3 * NT], in_=res[:, 2 * NT : 3 * NT])
-        scale_v(1)
-        scale_v(3)

@@ -112,22 +112,17 @@ def tile_pinsageconv_w_kernel(tc, h_node, h_ngbrs, alpha, Wq_words, Wq_scales, b
                     out=wq[:, g, lo:hi],
                     in_=Wq_words[g, :, lo:hi, :].rearrange("p n t -> p (n t)").bitcast(I32),
                 )
-        for q in (0, 2, 1, 3):
-            nc.sync.dma_start(
-                out=ww_pl[32 * q : 32 * q + 32, 0, :].bitcast(I32),
-                in_=Ww_scales[:, 4 * q : 4 * q + 4, :].bitcast(I32),
-            )
+        for hh in range(2):
+            for q in (0, 2, 1, 3):
+                nc.sync.dma_start(
+                    out=ww_pl[32 * q : 32 * q + 16, hh, :].bitcast(I32),
+                    in_=Ww_scales[4 * hh : 4 * hh + 4, 4 * q : 4 * q + 4, :].bitcast(I32),
+                )
         pieces = [(g, 0, FEAT) for g in range(4)] + [(4, 0, 1536)]
         pieces += [(g, lo, hi) for lo, hi in GROUPS[:3] for g in range(5, GW)]
         pieces += [(4, 1536, FEAT)]
         pieces += [(g, lo, hi) for lo, hi in GROUPS[3:] for g in range(5, GW)]
-        for n, (g, lo, hi) in enumerate(pieces):
-            if n == 3:
-                for q in (0, 2, 1, 3):
-                    nc.sync.dma_start(
-                        out=ww_pl[32 * q : 32 * q + 16, 1, :].bitcast(I32),
-                        in_=ww_pl[32 * q + 16 : 32 * q + 32, 0, :].bitcast(I32),
-                    )
+        for g, lo, hi in pieces:
             nc.sync.dma_start(
                 out=ww[:, g, lo:hi],
                 in_=Ww_words[g, :, lo:hi, :].rearrange("p n t -> p (n t)").bitcast(I32),
@@ -307,10 +302,9 @@ def tile_pinsageconv_w_kernel(tc, h_node, h_ngbrs, alpha, Wq_words, Wq_scales, b
         nc.scalar.activation(out=rn[:], in_=sq_all[:], func=ACT.Abs_reciprocal_sqrt, bias=ss_rest[:, 0:1], scale=1.0)
         lrelu(h2[:, 3 * NT : FEAT], v_end[:])
 
-        for c in range(4):
-            cols = slice(c * NT, (c + 1) * NT)
-            if c == 2:
-                nc.scalar.activation(out=res[:, cols], in_=h2[:, cols], func=ACT.Copy, scale=rn[:, 0:1])
+        for lo, hi, scalar in ((0, 256, False), (256, 768, False), (768, 1280, False), (1280, 1664, True), (1664, 2048, False)):
+            if scalar:
+                nc.scalar.activation(out=res[:, lo:hi], in_=h2[:, lo:hi], func=ACT.Copy, scale=rn[:, 0:1])
             else:
-                nc.vector.tensor_scalar(out=res[:, cols], in0=h2[:, cols], scalar1=rn[:, 0:1], scalar2=None, op0=ALU.mult)
-            nc.sync.dma_start(out=out[:, cols], in_=res[:, cols])
+                nc.vector.tensor_scalar(out=res[:, lo:hi], in0=h2[:, lo:hi], scalar1=rn[:, 0:1], scalar2=None, op0=ALU.mult)
+            nc.sync.dma_start(out=out[:, lo:hi], in_=res[:, lo:hi])

from contextlib import ExitStack

import concourse.bass as bass
import concourse.mybir as mybir
import concourse.tile as tile
from concourse.masks import make_identity

F32 = mybir.dt.float32
BF16 = mybir.dt.bfloat16
I32 = mybir.dt.int32
U32 = mybir.dt.uint32
U8 = mybir.dt.uint8
FP8X4 = mybir.dt.float8_e4m3fn_x4
ALU = mybir.AluOpType
ACT = mybir.ActivationFunctionType

P = 128
FEAT = 2048
NB = 2
K_PASS = 512
GQ = FEAT // K_PASS
GW = 2 * FEAT // K_PASS
NT = 512
WQ_CUTS = (0, 512, 1024, 2048)
ACC2_BANK = (4, 5, 2, 3, 6)
GROUPS = ((0, 512), (512, 1024), (1024, 1536), (1536, 1792), (1792, 2048))
SLOPE = 0.01
TINY = 1e-30

FLOPS = 2 * P * NB * FEAT * FEAT + 2 * P * 2 * FEAT * FEAT


def tile_pinsageconv_w_kernel(tc, h_node, h_ngbrs, alpha, Wq_words, Wq_scales, bq, Ww_words, Ww_scales, bw, out):
    nc = tc.nc
    with ExitStack() as ctx:
        ctx.enter_context(tc.manual_schedule(engines={mybir.EngineType.PE}))
        keep = ctx.enter_context(tc.tile_pool(name="keep", bufs=1))
        work = ctx.enter_context(tc.tile_pool(name="work", bufs=2))
        psum = ctx.enter_context(tc.psum_pool(name="psum", bufs=1))

        def bank(i, shape, dtype, name):
            return psum.tile(shape, dtype, tag="bank%d" % i, name=name)

        wq = keep.tile([P, GQ, FEAT], I32, align_bytes=64)
        ww = keep.tile([P, GW, FEAT], I32, align_bytes=64)
        wq_pl = keep.tile([P, FEAT], U8, align_bytes=64)
        ww_pl = keep.tile([P, 2, FEAT], U8, align_bytes=64)
        xn = keep.tile([P, NB, FEAT], BF16, align_bytes=64)
        xh = keep.tile([P, FEAT], BF16, align_bytes=64)
        gx = keep.tile([P, NB * GQ, P, 4], BF16, align_bytes=64)
        gh = keep.tile([P, GQ, P, 4], BF16, align_bytes=64)
        ga = keep.tile([P, GQ, P, 4], BF16, align_bytes=64)
        cx = keep.tile([P, NB * GQ * P], U32, align_bytes=64)
        ch = keep.tile([P, GQ * P], U32, align_bytes=64)
        ca = keep.tile([P, GQ * P], U32, align_bytes=64)
        px = keep.tile([P, NB * GQ * P], U8, align_bytes=64)
        ph = keep.tile([P, GQ * P], U8, align_bytes=64)
        pa = keep.tile([P, GQ * P], U8, align_bytes=64)
        ident_f = keep.tile([P, P], F32)
        ident_b = keep.tile([P, P], BF16)
        brow = keep.tile([P, NT], BF16)
        zeros = keep.tile([P, NT], BF16)
        bias_b = keep.tile([P, 2 * FEAT], BF16)
        a_bf = keep.tile([P, NB], BF16)
        a_f = keep.tile([P, NB], F32)
        a_sum = keep.tile([P, 1], F32)
        a_safe = keep.tile([P, 1], F32)
        a_rec = keep.tile([P, 1], F32)
        wgt = keep.tile([P, NB], F32)
        one = keep.tile([P, 1], F32)
        warm = keep.tile([P, 1], F32)
        hagg = keep.tile([P, FEAT], BF16)
        h2 = keep.tile([P, FEAT], F32)
        res = keep.tile([P, FEAT], F32)
        ssp = keep.tile([P, 4], F32)
        sq_all = keep.tile([P, 1], F32)
        sq_pos = keep.tile([P, 1], F32)
        ss_rest = keep.tile([P, 1], F32)
        junk = keep.tile([P, NT], F32)
        junk_v = keep.tile([P, NT], F32)
        v_end = keep.tile([P, NT], F32)
        ssprev = keep.tile([P, 1], F32)
        rn = keep.tile([P, 1], F32)

        nc.vector.memset(brow[:], 0.0)
        nc.vector.memset(one[:], 1.0)
        nc.vector.memset(zeros[:], 0.0)
        nc.vector.memset(ssp[:, 3:4], TINY)
        nc.vector.memset(wq_pl[:].bitcast(I32), 0)
        nc.vector.memset(ww_pl[:].rearrange("p h n -> p (h n)").bitcast(I32), 0)
        make_identity(nc, ident_b[:])
        make_identity(nc, ident_f[:])

        nc.scalar.dma_start(out=brow[0:4, :], in_=bq.rearrange("(c n) -> c n", c=4))
        nc.scalar.dma_start(out=brow[4:8, :], in_=bw.rearrange("(c n) -> c n", c=4))
        nc.scalar.dma_start(out=a_bf[:], in_=alpha.rearrange("n k o -> n (k o)"))
        nc.scalar.activation(out=warm[:], in_=one[:], func=ACT.Abs_reciprocal_sqrt)

        for hf in range(2):
            half = slice(hf * FEAT // 2, (hf + 1) * FEAT // 2)
            nc.sync.dma_start(out=xn[:, :, half], in_=h_ngbrs[:, :, half])
        for q in (0, 2, 1, 3):
            nc.sync.dma_start(
                out=wq_pl[32 * q : 32 * q + 16, :].bitcast(I32),
                in_=Wq_scales[:, 4 * q : 4 * q + 4, :].bitcast(I32),
            )
        for lo, hi in zip(WQ_CUTS, WQ_CUTS[1:]):
            if lo == WQ_CUTS[2]:
                nc.sync.dma_start(out=xh[:], in_=h_node)
            for g in range(GQ):
                nc.sync.dma_start(
                    out=wq[:, g, lo:hi],
                    in_=Wq_words[g, :, lo:hi, :].rearrange("p n t -> p (n t)").bitcast(I32),
                )
        for hh in range(2):
            for q in (0, 2, 1, 3):
                nc.sync.dma_start(
                    out=ww_pl[32 * q : 32 * q + 16, hh, :].bitcast(I32),
                    in_=Ww_scales[4 * hh : 4 * hh + 4, 4 * q : 4 * q + 4, :].bitcast(I32),
                )
        pieces = [(g, 0, FEAT) for g in range(4)] + [(4, 0, 1536)]
        pieces += [(g, lo, hi) for lo, hi in GROUPS[:3] for g in range(5, GW)]
        pieces += [(4, 1536, FEAT)]
        pieces += [(g, lo, hi) for lo, hi in GROUPS[3:] for g in range(5, GW)]
        for g, lo, hi in pieces:
            nc.sync.dma_start(
                out=ww[:, g, lo:hi],
                in_=Ww_words[g, :, lo:hi, :].rearrange("p n t -> p (n t)").bitcast(I32),
            )

        def bias_matmul(j, b):
            pb = bank(b, [P, 2, NT], BF16, "pb%d" % j)
            for r in range(2):
                row = 2 * j + r
                nc.tensor.matmul(out=pb[:, r, :], lhsT=ident_b[:, row : row + 1].to_broadcast([P, P]), rhs=brow[:], start=True, stop=True)
            return pb

        def bias_evac(j, pb):
            nc.scalar.copy(out=bias_b[:, 2 * j * NT : 2 * (j + 1) * NT], in_=pb[:].rearrange("p r n -> p (r n)"))

        def word_transposes(src_words, b, bases, name):
            pt = bank(b, [P, 2, 2, P], F32, name)
            for a in range(2):
                for u in range(2):
                    nc.tensor.transpose(pt[:, a, u, :], src_words[:, bases[a] + u : bases[a] + 256 : 2], ident_f[:])
            return pt

        def word_evac(eng_copy, dst, unit0, pt):
            eng_copy(
                out=dst[:, unit0 : unit0 + 2, :, :].bitcast(F32),
                in_=pt[:].rearrange("p a u r -> p a r u"),
            )

        def quantise(src, codes, plane, unit0, units):
            nc.vector.quantize_mx(
                out=codes[:, unit0 * P : (unit0 + units) * P].bitcast(FP8X4),
                scales=plane[:, unit0 * P : (unit0 + units) * P],
                in_=src[:, unit0 : unit0 + units, :, :].rearrange("p a r t -> p (a r t)"),
            )

        idle = bank(7, [P, NT], F32, "idle")
        for i in range(3):
            nc.tensor.matmul(out=idle[:], lhsT=ident_b[:], rhs=zeros[:], start=True, stop=True)

        xnw = xn[:].rearrange("p k f -> p (k f)").bitcast(F32)
        for g in range(GQ):
            tx = word_transposes(xnw, g, [kk * FEAT // 2 + 256 * g for kk in range(NB)], "tx%d" % g)
            word_evac(nc.vector.tensor_copy if g % 2 == 0 else nc.scalar.copy, gx, NB * g, tx)
            quantise(gx, cx, px, NB * g, NB)
        nc.vector.tensor_copy(out=a_f[:], in_=a_bf[:])
        nc.vector.tensor_tensor(out=a_sum[:], in0=a_f[:, 0:1], in1=a_f[:, 1:2], op=ALU.add)
        nc.vector.scalar_tensor_tensor(out=a_safe[:], in0=a_sum[:], scalar=0.0, in1=a_sum[:], op0=ALU.is_equal, op1=ALU.add)
        nc.vector.reciprocal(out=a_rec[:], in_=a_safe[:])
        nc.vector.tensor_scalar(out=wgt[:], in0=a_f[:], scalar1=a_rec[:, 0:1], scalar2=None, op0=ALU.mult)

        acc1 = {}

        def passes1(lo, hi):
            js = range(lo // NT, hi // NT)
            for j in js:
                for kk in range(NB):
                    acc1[(j, kk)] = bank(2 * j + kk, [P, NT], F32, "acc1_%d%d" % (j, kk))
            for j in js:
                for g in range(GQ):
                    for kk in range(NB):
                        unit = NB * g + kk
                        nc.tensor.matmul_mx(
                            out=acc1[(j, kk)][:],
                            lhsT=cx[:, unit * P : (unit + 1) * P].bitcast(FP8X4),
                            lhsT_scale=px[:, unit * P : (unit + 1) * P],
                            rhs=wq[:, g, j * NT : (j + 1) * NT].bitcast(FP8X4),
                            rhs_scale=wq_pl[4 * g : P, j * NT : (j + 1) * NT],
                            start=(g == 0),
                            stop=(g == GQ - 1),
                        )

        def lrelu(dst, v):
            nc.vector.scalar_tensor_tensor(out=dst, in0=v, scalar=SLOPE, in1=v, op0=ALU.mult, op1=ALU.max)

        vs, us, ys = {}, {}, {}

        def e_add(j):
            vs[j] = work.tile([P, NB, NT], F32, tag="v", name="v%d" % j)
            for kk in range(NB):
                nc.vector.tensor_tensor(out=vs[j][:, kk, :], in0=acc1[(j, kk)][:], in1=bias_b[:, j * NT : (j + 1) * NT], op=ALU.add)

        def e_lrelu_mul(j):
            us[j] = work.tile([P, NB, NT], F32, tag="u", name="u%d" % j)
            ys[j] = work.tile([P, NT], F32, tag="y", name="y%d" % j)
            lrelu(us[j][:].rearrange("p k n -> p (k n)"), vs[j][:].rearrange("p k n -> p (k n)"))
            nc.scalar.activation(out=ys[j][:], in_=us[j][:, 0, :], func=ACT.Copy, scale=wgt[:, 0:1])

        def e_fma_transpose(j):
            nc.vector.scalar_tensor_tensor(out=hagg[:, j * NT : (j + 1) * NT], in0=us[j][:, 1, :], scalar=wgt[:, 1:2], in1=ys[j][:], op0=ALU.mult, op1=ALU.add)
            pt = bank(j % 2, [P, 4, P], BF16, "ta%d" % j)
            for t in range(4):
                nc.tensor.transpose(pt[:, t, :], hagg[:, K_PASS * j + t : K_PASS * (j + 1) : 4], ident_b[:])
            nc.scalar.copy(out=ga[:, j, :, :], in_=pt[:].rearrange("p t r -> p r t"))

        acc2 = {}
        seen = [0] * len(GROUPS)

        def pass2(g, j):
            lo, hi = GROUPS[j]
            if j not in acc2:
                acc2[j] = bank(ACC2_BANK[j], [P, hi - lo], F32, "acc2_%d" % j)
            if g < GQ:
                codes, plane, unit = ch, ph, g
            else:
                codes, plane, unit = ca, pa, g - GQ
            nc.tensor.matmul_mx(
                out=acc2[j][:],
                lhsT=codes[:, unit * P : (unit + 1) * P].bitcast(FP8X4),
                lhsT_scale=plane[:, unit * P : (unit + 1) * P],
                rhs=ww[:, g, lo:hi].bitcast(FP8X4),
                rhs_scale=ww_pl[4 * (g % 4) : P, g // 4, lo:hi],
                start=(seen[j] == 0),
                stop=(seen[j] == GW - 1),
            )
            seen[j] += 1

        def passes(first, end):
            for g, lo, hi in pieces[first:end]:
                for j, (glo, ghi) in enumerate(GROUPS):
                    if lo <= glo and ghi <= hi:
                        pass2(g, j)

        bias_evac(0, bias_matmul(0, 4))
        passes1(0, 512)
        bias_evac(1, bias_matmul(1, 5))
        passes1(512, 1024)
        for j in range(2, 4):
            bias_evac(j, bias_matmul(j, 4 + j))
        e_add(0)
        e_lrelu_mul(0)
        xhw = xh[:].bitcast(F32)
        t4 = word_transposes(xhw, 0, (0, 256), "t4")
        t5 = word_transposes(xhw, 1, (512, 768), "t5")
        word_evac(nc.scalar.copy, gh, 0, t4)
        word_evac(nc.scalar.copy, gh, 2, t5)
        passes1(1024, 1536)
        e_add(1)
        e_fma_transpose(0)
        passes1(1536, 2048)
        e_lrelu_mul(1)
        quantise(gh, ch, ph, 0, 4)
        e_add(2)
        e_fma_transpose(1)
        quantise(ga, ca, pa, 0, 1)
        passes(0, 2)
        e_lrelu_mul(2)
        e_add(3)
        quantise(ga, ca, pa, 1, 1)
        e_fma_transpose(2)
        passes(2, 3)
        e_lrelu_mul(3)
        quantise(ga, ca, pa, 2, 1)
        e_fma_transpose(3)
        passes(3, 4)
        quantise(ga, ca, pa, 3, 1)
        passes(4, len(pieces))

        ctx.enter_context(tc.manual_schedule())

        def add2(dst, j):
            lo, hi = GROUPS[j]
            nc.vector.tensor_tensor(out=dst, in0=acc2[j][:], in1=bias_b[:, FEAT + lo : FEAT + hi], op=ALU.add)

        for j in range(3):
            lo, hi = GROUPS[j]
            v = work.tile([P, NT], F32, tag="v2")
            add2(v[:], j)
            lrelu(h2[:, lo:hi], v[:])
            nc.scalar.activation(out=junk[:], in_=h2[:, lo:hi], func=ACT.Square, accum_out=ssp[:, j : j + 1])

        add2(v_end[:, 0:256], 3)
        add2(v_end[:, 256:512], 4)
        nc.scalar.activation(out=junk[:], in_=v_end[:], func=ACT.Square, scale=SLOPE, accum_out=sq_all[:])
        nc.vector.scalar_tensor_tensor(out=junk_v[:], in0=v_end[:], scalar=0.0, in1=v_end[:], op0=ALU.max, op1=ALU.mult, accum_out=sq_pos[:])
        nc.vector.tensor_reduce(out=ssprev[:], in_=ssp[:], op=ALU.add, axis=mybir.AxisListType.X)
        nc.vector.scalar_tensor_tensor(out=ss_rest[:], in0=sq_pos[:], scalar=1.0 - SLOPE * SLOPE, in1=ssprev[:], op0=ALU.mult, op1=ALU.add)
        nc.scalar.activation(out=rn[:], in_=sq_all[:], func=ACT.Abs_reciprocal_sqrt, bias=ss_rest[:, 0:1], scale=1.0)
        lrelu(h2[:, 3 * NT : FEAT], v_end[:])

        for lo, hi, scalar in ((0, 256, False), (256, 768, False), (768, 1280, False), (1280, 1664, True), (1664, 2048, False)):
            if scalar:
                nc.scalar.activation(out=res[:, lo:hi], in_=h2[:, lo:hi], func=ACT.Copy, scale=rn[:, 0:1])
            else:
                nc.vector.tensor_scalar(out=res[:, lo:hi], in0=h2[:, lo:hi], scalar1=rn[:, 0:1], scalar2=None, op0=ALU.mult)
            nc.sync.dma_start(out=out[:, lo:hi], in_=res[:, lo:hi])
